import numpy as np
import ml_dtypes


def mxq(x, axis, fmt="e4m3"):
    dtype, down = {"e4m3": (ml_dtypes.float8_e4m3fn, 7), "e5m2": (ml_dtypes.float8_e5m2, 14)}[fmt]
    v = np.moveaxis(np.asarray(x, np.float32).astype(ml_dtypes.bfloat16).astype(np.float64), axis, -1)
    blocks = v.reshape(v.shape[:-1] + (-1, 32))
    amax = np.abs(blocks).max(-1, keepdims=True)
    byte = np.maximum(np.where(amax > 0, np.frexp(amax)[1] - 1 + 127, 0) - down, 1)
    scale = np.exp2(byte - 127.0)
    codes = (blocks / scale).astype(np.float32).astype(dtype).astype(np.float64)
    return np.moveaxis((codes * scale).reshape(v.shape), -1, axis)


WIDE = False


def mx_kscale(k):
    if not WIDE:
        return np.ones(k)
    levels = np.array([10, -10, 5, -5, 0])
    if k % 512:
        return np.exp2(np.random.permutation(np.resize(levels, k // 32))).repeat(32)
    a = np.empty((k // 512, 16))
    for p in range(k // 512):
        a[p, :8] = np.random.permutation(np.resize(levels, 8))
        for g in range(8):
            far = levels[np.abs(levels - a[p, g]) >= 10]
            a[p, g + 8] = far[np.random.randint(len(far))]
    return np.exp2(a.ravel()).repeat(32)


BF16 = ml_dtypes.bfloat16


def bf(x):
    return np.asarray(x, np.float32).astype(BF16)


def f64(x):
    return np.asarray(x).astype(np.float64)


B, H, W, WS, C, NH, DH, F, PT = 2, 56, 56, 14, 512, 4, 64, 2048, 16
E = NH * DH
N = WS * WS
GH, GW = H // WS, W // WS
BW = B * GH * GW
HALF = DH // 2
EPS = 1e-6
THETA = 10000.0


def layer_norm(v, w, b):
    mu = v.mean(-1, keepdims=True)
    var = ((v - mu) ** 2).mean(-1, keepdims=True)
    return (v - mu) / np.sqrt(var + EPS) * w + b


def rotate_half(u):
    ur = u.reshape(u.shape[:-1] + (-1, 2))
    return np.stack((-ur[..., 1], ur[..., 0]), -1).reshape(u.shape)


def rope_tables():
    freqs = 1.0 / THETA ** (np.arange(0, HALF, 2) / HALF)
    ang = np.repeat((np.arange(WS) / WS * PT)[:, None] * freqs[None, :], 2, axis=-1)
    f = np.concatenate([np.broadcast_to(ang[:, None, :], (WS, WS, HALF)),
                        np.broadcast_to(ang[None, :, :], (WS, WS, HALF))], -1).reshape(N, DH)
    return np.cos(f), np.sin(f)


def setup_inputs():
    s = mx_kscale(C)
    r = np.random.standard_normal
    return {"x": bf(1.5 * r((B, H, W, C)) + 0.5 * r((B, H, W, 1))),
            "ln1_w": bf((1.0 + 0.1 * r(C)) * s), "ln1_b": bf(0.2 * r(C) * s),
            "q_w": bf(r((C, E)) / np.sqrt(C) / s[:, None]), "q_b": bf(0.3 * r(E)),
            "k_w": bf(r((C, E)) / np.sqrt(C) / s[:, None]),
            "v_w": bf(r((C, E)) / np.sqrt(C) / s[:, None]), "v_b": bf(0.3 * r(E))}


def reference(x, ln1_w, ln1_b, q_w, q_b, k_w, v_w, v_b):
    h = layer_norm(f64(x), f64(ln1_w), f64(ln1_b))
    t = h.reshape(B, GH, WS, GW, WS, C).transpose(0, 1, 3, 2, 4, 5).reshape(BW, N, C)
    tq = mxq(t, 2, "e4m3")
    q = (tq @ mxq(f64(q_w), 0, "e4m3")) + f64(q_b)
    k = tq @ mxq(f64(k_w), 0, "e4m3")
    v = (tq @ mxq(f64(v_w), 0, "e4m3")) + f64(v_b)
    q = q.reshape(BW, N, NH, DH).transpose(0, 2, 1, 3)
    k = k.reshape(BW, N, NH, DH).transpose(0, 2, 1, 3)
    v = v.reshape(BW, N, NH, DH).transpose(0, 2, 1, 3)
    cos, sin = rope_tables()
    q = q * cos + rotate_half(q) * sin
    k = k * cos + rotate_half(k) * sin
    return q, k, v

@@ -1,0 +1,339 @@
+import math
+from contextlib import ExitStack
+
+import concourse.mybir as mybir
+from concourse.masks import make_identity
+
+F32 = mybir.dt.float32
+BF16 = mybir.dt.bfloat16
+I32 = mybir.dt.int32
+U32 = mybir.dt.uint32
+U8 = mybir.dt.uint8
+FP8X4 = mybir.dt.float8_e4m3fn_x4
+ALU = mybir.AluOpType
+ACT = mybir.ActivationFunctionType
+
+P = 128
+C = 512
+PACK = 4
+E = 256
+NH, DH = 4, 64
+HALF = DH // 2
+FREQS = HALF // 2
+WS = 14
+PT = 16.0
+THETA = 10000.0
+EPS = 1e-6
+GROUPS = 7
+RUN = 7
+TILES = GROUPS * RUN
+ROUND = 4
+ROUNDS = (TILES + ROUND - 1) // ROUND
+W_COLS = 5 * E
+
+FLOPS = 2 * 6272 * C * 3 * E
+
+
+def quantise_weights(nc, setup, keep, q_w, k_w, v_w):
+    raw = setup.tile([P, 3, PACK, E], BF16)
+    for n, w in enumerate((q_w, k_w, v_w)):
+        nc.scalar.dma_start(out=raw[:, n], in_=w.rearrange("(p j) e -> p j e", j=PACK))
+    grouped = setup.tile([P, W_COLS, PACK], BF16, align_bytes=64)
+    for n, first in enumerate((0, 2 * E, 4 * E)):
+        nc.vector.tensor_copy(
+            out=grouped[:, first : first + E, :], in_=raw[:, n].rearrange("p j e -> p e j")
+        )
+    for n, first in enumerate((E, 3 * E)):
+        dst = grouped[:, first : first + E, :].rearrange("p (m e) j -> p m e j", e=2)
+        src = raw[:, n].rearrange("p j (m e) -> p m e j", e=2)
+        for e in range(2):
+            nc.vector.tensor_copy(out=dst[:, :, e, :], in_=src[:, :, 1 - e, :])
+    w_codes = keep.tile([P, W_COLS], U32, align_bytes=64)
+    w_scales = keep.tile([P, W_COLS], U8, align_bytes=64)
+    for first, last in ((0, 4 * E), (4 * E, 5 * E)):
+        nc.vector.quantize_mx(
+            out=w_codes[:, first:last].bitcast(FP8X4),
+            scales=w_scales[:, first:last],
+            in_=grouped[:, first:last, :].rearrange("p e j -> p (e j)"),
+        )
+    return w_codes, w_scales
+
+
+def layer_norm_columns(nc, setup, keep, ln1_w, ln1_b):
+    ln_cols = keep.tile([P, 2 * PACK], F32)
+    for n, vec in enumerate((ln1_w, ln1_b)):
+        cols_bf = setup.tile([P, PACK], BF16)
+        nc.scalar.dma_start(out=cols_bf[:], in_=vec.rearrange("(p j) -> p j", j=PACK))
+        nc.vector.tensor_copy(out=ln_cols[:, n * PACK : (n + 1) * PACK], in_=cols_bf[:])
+    return ln_cols
+
+
+def rotary_tables(nc, setup, keep, q_b):
+    part_i = setup.tile([P, 1], I32)
+    nc.gpsimd.iota(part_i[:], pattern=[[0, 1]], base=0, channel_multiplier=1)
+    step_i = setup.tile([P, RUN], I32)
+    nc.gpsimd.iota(step_i[:], pattern=[[1, RUN]], base=0, channel_multiplier=0)
+    row_i = setup.tile([P, 1], I32)
+    nc.vector.tensor_scalar(
+        out=row_i[:], in0=part_i[:], scalar1=1, scalar2=1,
+        op0=ALU.logical_shift_right, op1=ALU.bitwise_and,
+    )
+    half_i = setup.tile([P, 1], I32)
+    nc.vector.tensor_single_scalar(out=half_i[:], in_=part_i[:], scalar=1, op=ALU.bitwise_and)
+    row_f = setup.tile([P, 1], F32)
+    nc.vector.tensor_copy(out=row_f[:], in_=row_i[:])
+    half_f = setup.tile([P, 1], F32)
+    nc.vector.tensor_copy(out=half_f[:], in_=half_i[:])
+    step_f = setup.tile([P, RUN], F32)
+    nc.vector.tensor_copy(out=step_f[:], in_=step_i[:])
+    col0_f = setup.tile([P, 1], F32)
+    nc.vector.tensor_scalar_mul(out=col0_f[:], in0=half_f[:], scalar1=float(RUN))
+    pos = setup.tile([P, 2 * RUN], F32)
+    nc.vector.tensor_scalar(
+        out=pos[:, 0:GROUPS], in0=step_f[:], scalar1=2.0, scalar2=row_f[:, 0:1],
+        op0=ALU.mult, op1=ALU.add,
+    )
+    nc.vector.tensor_scalar_add(out=pos[:, GROUPS:], in0=step_f[:], scalar1=col0_f[:, 0:1])
+    arg = setup.tile([P, 2, 2 * RUN, FREQS], F32)
+    for m in range(FREQS):
+        nc.vector.tensor_scalar_mul(
+            out=arg[:, 1, :, m], in0=pos[:], scalar1=PT / WS * THETA ** (-m / FREQS)
+        )
+    nc.vector.tensor_scalar_add(out=arg[:, 0], in0=arg[:, 1], scalar1=math.pi / 2)
+    largest = (WS - 1) * PT / WS + math.pi / 2
+    for turn in range(math.ceil((largest - math.pi) / (2 * math.pi))):
+        wrap = setup.tile([P, 2, 2 * RUN, FREQS], F32)
+        nc.vector.tensor_scalar(
+            out=wrap[:], in0=arg[:], scalar1=math.pi, scalar2=-2 * math.pi,
+            op0=ALU.is_gt, op1=ALU.mult,
+        )
+        nc.vector.tensor_tensor(out=arg[:], in0=arg[:], in1=wrap[:], op=ALU.add)
+    cos_sin = setup.tile([P, 2, 2 * RUN, FREQS], F32)
+    nc.scalar.activation(out=cos_sin[:], in_=arg[:], func=ACT.Sin)
+    paired = setup.tile([P, 2, 2 * RUN, HALF], F32)
+    pairs = paired[:].rearrange("p k n (m e) -> p k n m e", e=2)
+    for e in range(2):
+        nc.vector.tensor_copy(out=pairs[:, 0, :, :, e], in_=cos_sin[:, 0])
+    nc.vector.tensor_scalar_mul(out=pairs[:, 1, :, :, 0], in0=cos_sin[:, 1], scalar1=-1.0)
+    nc.vector.tensor_copy(out=pairs[:, 1, :, :, 1], in_=cos_sin[:, 1])
+    table = keep.tile([P, TILES, 2, DH], F32)
+    by_group = table[:].rearrange("p (s c) k d -> p s c k d", c=RUN)
+    shape = [P, GROUPS, RUN, HALF]
+    for k in range(2):
+        nc.gpsimd.tensor_scalar(
+            out=by_group[:, :, :, k, 0:HALF],
+            in0=paired[:, k, 0:GROUPS].unsqueeze(2).to_broadcast(shape),
+            scalar1=1.0, scalar2=0.0, op0=ALU.mult, op1=ALU.add,
+        )
+        nc.gpsimd.tensor_scalar(
+            out=by_group[:, :, :, k, HALF:DH],
+            in0=paired[:, k, GROUPS:].unsqueeze(1).to_broadcast(shape),
+            scalar1=1.0, scalar2=0.0, op0=ALU.mult, op1=ALU.add,
+        )
+    bias_bf = setup.tile([P, E], BF16)
+    nc.scalar.dma_start(out=bias_bf[:], in_=q_b.partition_broadcast(P))
+    bias = setup.tile([P, 2, NH, DH], F32)
+    nc.vector.tensor_copy(out=bias[:, 0], in_=bias_bf[:].rearrange("p (h d) -> p h d", h=NH))
+    src = bias_bf[:].rearrange("p (h m e) -> p h m e", h=NH, e=2)
+    dst = bias[:, 1].rearrange("p h (m e) -> p h m e", e=2)
+    for e in range(2):
+        nc.vector.tensor_copy(out=dst[:, :, :, e], in_=src[:, :, :, 1 - e])
+    q_rot = keep.tile([P, 2 * RUN, NH, HALF], F32)
+    shape = [P, RUN, NH, HALF]
+    for axis in range(2):
+        n0, d0 = axis * RUN, axis * HALF
+        term0 = setup.tile([P, RUN, NH, HALF], F32)
+        term1 = setup.tile([P, RUN, NH, HALF], F32)
+        for k, term in enumerate((term0, term1)):
+            nc.gpsimd.tensor_tensor(
+                out=term[:],
+                in0=bias[:, k, :, d0 : d0 + HALF].unsqueeze(1).to_broadcast(shape),
+                in1=paired[:, k, n0 : n0 + RUN].unsqueeze(2).to_broadcast(shape),
+                op=ALU.mult,
+            )
+        nc.gpsimd.tensor_tensor(
+            out=q_rot[:, n0 : n0 + RUN], in0=term0[:], in1=term1[:], op=ALU.add
+        )
+    return table, q_rot
+
+
+def tile_block_pa_t_kernel(
+    tc, x, ln1_w, ln1_b, q_w, q_b, k_w, v_w, v_b, out_0, out_1, out_2
+):
+    nc = tc.nc
+    with ExitStack() as ctx:
+        keep = ctx.enter_context(tc.tile_pool(name="keep", bufs=1))
+        work = ctx.enter_context(tc.tile_pool(name="work", bufs=2))
+        small = ctx.enter_context(tc.tile_pool(name="small", bufs=4))
+        psum_t = ctx.enter_context(tc.psum_pool(name="psum_t", bufs=3))
+        psum_mx = ctx.enter_context(tc.psum_pool(name="psum_mx", bufs=5))
+
+        x_sb = keep.tile([P, TILES, C], BF16)
+        x_groups = x.flatten_outer_dims().rearrange(
+            "(bi s g c) ch -> s g bi (c ch)", bi=8, s=GROUPS, g=16, c=RUN
+        )
+        for s in range(GROUPS):
+            nc.sync.dma_start(
+                out=x_sb[:, s * RUN : (s + 1) * RUN, :].rearrange("p c ch -> p (c ch)"),
+                in_=x_groups[s],
+            )
+
+        with tc.tile_pool(name="setup", bufs=1) as setup:
+            ident = setup.tile([P, P], F32)
+            make_identity(nc, ident[:])
+            perm = keep.tile([P, P], F32)
+            nc.vector.tensor_copy(
+                out=perm[:].rearrange("p (bi j rl hf) -> p bi j rl hf", bi=8, j=4, rl=2, hf=2),
+                in_=ident[:].rearrange("p (rl j hf bi) -> p bi j rl hf", rl=2, j=4, hf=2, bi=8),
+            )
+            ln_cols = layer_norm_columns(nc, setup, keep, ln1_w, ln1_b)
+            w_codes, w_scales = quantise_weights(nc, setup, keep, q_w, k_w, v_w)
+            table, q_rot = rotary_tables(nc, setup, keep, q_b)
+            vb_bf = setup.tile([P, E], BF16)
+            nc.scalar.dma_start(out=vb_bf[:], in_=v_b.partition_broadcast(P))
+            v_bias = keep.tile([P, NH, DH], F32)
+            nc.vector.tensor_copy(out=v_bias[:], in_=vb_bf[:].rearrange("p (h d) -> p h d", h=NH))
+            eps = keep.tile([P, 1], F32)
+            nc.vector.memset(eps[:], EPS)
+
+        stage = ctx.enter_context(tc.tile_pool(name="stage", bufs=2))
+        outs = [
+            o.rearrange("w h (s q c) d -> s h w q (c d)", s=GROUPS, q=4, c=RUN)
+            for o in (out_0, out_1, out_2)
+        ]
+        scale_of, codes_of, stage_of = {}, {}, {}
+
+        def tiles_of(r):
+            return range(r * ROUND, min((r + 1) * ROUND, TILES))
+
+        def statistics(r):
+            n = len(tiles_of(r))
+            six = small.tile([P, ROUND, 6], F32)
+            mean_var = small.tile([P, ROUND, 2], F32)
+            for i, t in enumerate(tiles_of(r)):
+                nc.vector.bn_stats(out=six[:, i, :], in_=x_sb[:, t, :])
+            for i in range(n):
+                nc.vector.bn_aggr(out=mean_var[:, i, :], in_=six[:, i, :])
+            std = small.tile([P, ROUND], F32)
+            nc.scalar.activation(
+                out=std[:, 0:n], in_=mean_var[:, 0:n, 1], func=ACT.Sqrt, bias=eps[:, 0:1], scale=1.0
+            )
+            rstd = small.tile([P, ROUND], F32)
+            nc.vector.reciprocal(out=rstd[:, 0:n], in_=std[:, 0:n])
+            shift = small.tile([P, ROUND], F32)
+            nc.vector.scalar_tensor_tensor(
+                out=shift[:, 0:n], in0=mean_var[:, 0:n, 0], scalar=-1.0, in1=rstd[:, 0:n],
+                op0=ALU.mult, op1=ALU.mult,
+            )
+            scale_of[r] = (rstd, shift)
+
+        def normalise_and_transpose(r):
+            n = len(tiles_of(r))
+            rstd, shift = scale_of[r]
+            xn = work.tile([P, ROUND, C], F32)
+            for i, t in enumerate(tiles_of(r)):
+                nc.scalar.activation(
+                    out=xn[:, i, :].rearrange("p (j k) -> p j k", j=PACK),
+                    in_=x_sb[:, t, :].rearrange("p (k j) -> p j k", j=PACK), func=ACT.Identity,
+                    bias=shift[:, i : i + 1], scale=rstd[:, i : i + 1],
+                )
+            planes = work.tile([P, PACK, ROUND * P], BF16)
+            for j in range(PACK):
+                xt = psum_t.tile([P, ROUND * P], F32, tag="xt")
+                for i in range(n):
+                    nc.tensor.transpose(
+                        xt[:, i * P : (i + 1) * P], xn[:, i, j * P : (j + 1) * P], perm[:]
+                    )
+                nc.scalar.activation(
+                    out=planes[:, j, 0 : n * P], in_=xt[:, 0 : n * P], func=ACT.Identity,
+                    bias=ln_cols[:, PACK + j : PACK + j + 1], scale=ln_cols[:, j : j + 1],
+                )
+            grouped = work.tile([P, ROUND * P, PACK], BF16, align_bytes=64)
+            nc.scalar.copy(
+                out=grouped[:, 0 : n * P, :].rearrange("p (c i) j -> p c j i", i=4),
+                in_=planes[:, :, 0 : n * P].rearrange("p j (c i) -> p c j i", i=4),
+            )
+            codes_of[r] = grouped
+
+        def project_and_rotate(r):
+            n = len(tiles_of(r))
+            grouped = codes_of[r]
+            codes = work.tile([P, ROUND * P], U32, align_bytes=64)
+            scales = work.tile([P, ROUND * P], U8, align_bytes=64)
+            nc.vector.quantize_mx(
+                out=codes[:, 0 : n * P].bitcast(FP8X4),
+                scales=scales[:, 0 : n * P],
+                in_=grouped[:, 0 : n * P, :].rearrange("p t j -> p (t j)"),
+            )
+            for i, t in enumerate(tiles_of(r)):
+                s, c = divmod(t, RUN)
+                if c == 0:
+                    qk_new = stage.tile([P, 2, 2, NH, RUN, DH], F32, name="qk_stage")
+                    v_new = stage.tile([P, NH, RUN, DH], F32, name="v_stage")
+                    stage_of[s] = (qk_new, v_new)
+                qk_stage, v_stage = stage_of[s]
+                tokens = slice(i * P, (i + 1) * P)
+                for n_out in range(2):
+                    acc = psum_mx.tile([P, 2 * E], F32, tag="mx")
+                    cols = slice(n_out * 2 * E, (n_out + 1) * 2 * E)
+                    nc.tensor.matmul_mx(
+                        out=acc[:],
+                        lhsT=codes[:, tokens].bitcast(FP8X4), lhsT_scale=scales[:, tokens],
+                        rhs=w_codes[:, cols].bitcast(FP8X4), rhs_scale=w_scales[:, cols],
+                        start=True, stop=True,
+                    )
+                    nc.vector.tensor_tensor(
+                        out=qk_stage[:, n_out, :, :, c, :],
+                        in0=acc[:].rearrange("p (k h d) -> p k h d", k=2, h=NH),
+                        in1=table[:, t].unsqueeze(2).to_broadcast([P, 2, NH, DH]),
+                        op=ALU.mult,
+                    )
+                acc_v = psum_mx.tile([P, 2 * E], F32, tag="mx")
+                cols = slice(4 * E, 5 * E)
+                nc.tensor.matmul_mx(
+                    out=acc_v[:, 0:E],
+                    lhsT=codes[:, tokens].bitcast(FP8X4), lhsT_scale=scales[:, tokens],
+                    rhs=w_codes[:, cols].bitcast(FP8X4), rhs_scale=w_scales[:, cols],
+                    start=True, stop=True,
+                )
+                nc.vector.tensor_tensor(
+                    out=v_stage[:, :, c, :],
+                    in0=acc_v[:, 0:E].rearrange("p (h d) -> p h d", h=NH),
+                    in1=v_bias[:], op=ALU.add,
+                )
+                if c == RUN - 1:
+                    finish_group(s)
+
+        def finish_group(s):
+            qk_stage, v_stage = stage_of[s]
+            for h in range(NH):
+                nc.sync.dma_start(
+                    out=outs[2][s, h], in_=v_stage[:, h].rearrange("p c d -> p (c d)")
+                )
+            for n_out in range(2):
+                done = qk_stage[:, n_out, 0]
+                nc.gpsimd.tensor_tensor(
+                    out=done, in0=done, in1=qk_stage[:, n_out, 1], op=ALU.add
+                )
+                if n_out == 0:
+                    shape = [P, NH, RUN, HALF]
+                    nc.gpsimd.tensor_tensor(
+                        out=done[:, :, :, 0:HALF], in0=done[:, :, :, 0:HALF],
+                        in1=q_rot[:, s].unsqueeze(2).to_broadcast(shape), op=ALU.add,
+                    )
+                    nc.gpsimd.tensor_tensor(
+                        out=done[:, :, :, HALF:DH], in0=done[:, :, :, HALF:DH],
+                        in1=q_rot[:, GROUPS:].rearrange("p c h d -> p h c d"), op=ALU.add,
+                    )
+                for h in range(NH):
+                    nc.sync.dma_start(
+                        out=outs[n_out][s, h], in_=done[:, h].rearrange("p c d -> p (c d)")
+                    )
+
+        for step in range(ROUNDS + 2):
+            if step < ROUNDS:
+                statistics(step)
+            if 1 <= step <= ROUNDS:
+                normalise_and_transpose(step - 1)
+            if step >= 2:
+                project_and_rotate(step - 2)

@@ -24,33 +24,40 @@ WS = 14
 PT = 16.0
 THETA = 10000.0
 EPS = 1e-6
-GROUPS = 7
+ROWS = 4
+BANDS = 3
 RUN = 7
-TILES = GROUPS * RUN
-ROUND = 4
-ROUNDS = (TILES + ROUND - 1) // ROUND
-W_COLS = 5 * E
+TILES = BANDS * WS + RUN
+BANK = 512
 
 FLOPS = 2 * 6272 * C * 3 * E
 
 
-def quantise_weights(nc, setup, keep, q_w, k_w, v_w):
-    raw = setup.tile([P, 3, PACK, E], BF16)
-    for n, w in enumerate((q_w, k_w, v_w)):
-        nc.scalar.dma_start(out=raw[:, n], in_=w.rearrange("(p j) e -> p j e", j=PACK))
-    grouped = setup.tile([P, W_COLS, PACK], BF16, align_bytes=64)
-    for n, first in enumerate((0, 2 * E, 4 * E)):
-        nc.vector.tensor_copy(
-            out=grouped[:, first : first + E, :], in_=raw[:, n].rearrange("p j e -> p e j")
-        )
-    for n, first in enumerate((E, 3 * E)):
-        dst = grouped[:, first : first + E, :].rearrange("p (m e) j -> p m e j", e=2)
-        src = raw[:, n].rearrange("p j (m e) -> p m e j", e=2)
-        for e in range(2):
-            nc.vector.tensor_copy(out=dst[:, :, e, :], in_=src[:, :, 1 - e, :])
-    w_codes = keep.tile([P, W_COLS], U32, align_bytes=64)
-    w_scales = keep.tile([P, W_COLS], U8, align_bytes=64)
-    for first, last in ((0, 4 * E), (4 * E, 5 * E)):
+def units_of_tiles():
+    units = [(2 * u, 2) for u in range(BANDS * WS // 2)]
+    for i in range(0, RUN, 2):
+        units.append((BANDS * WS + i, min(2, RUN - i)))
+    return units
+
+
+def quantise_weights(nc, setup, keep, raws):
+    w_codes = keep.tile([P, 3 * E], U32, align_bytes=64)
+    w_scales = keep.tile([P, 3 * E], U8, align_bytes=64)
+    grouped = setup.tile([P, 3 * E, PACK], BF16, align_bytes=64)
+    for n, raw in enumerate(raws):
+        if n < 2:
+            src = raw[:].rearrange("p j (h f d) -> p f h d j", h=NH, f=2)
+            for f in range(2):
+                first = n * E + f * P
+                nc.vector.tensor_copy(
+                    out=grouped[:, first : first + P, :].rearrange("p (h d) j -> p h d j", h=NH),
+                    in_=src[:, f],
+                )
+        else:
+            nc.vector.tensor_copy(
+                out=grouped[:, 2 * E :, :], in_=raw[:].rearrange("p j e -> p e j")
+            )
+    for first, last in ((0, 2 * E), (2 * E, 3 * E)):
         nc.vector.quantize_mx(
             out=w_codes[:, first:last].bitcast(FP8X4),
             scales=w_scales[:, first:last],
@@ -59,102 +66,115 @@ def quantise_weights(nc, setup, keep, q_w, k_w, v_w):
     return w_codes, w_scales
 
 
-def layer_norm_columns(nc, setup, keep, ln1_w, ln1_b):
-    ln_cols = keep.tile([P, 2 * PACK], F32)
-    for n, vec in enumerate((ln1_w, ln1_b)):
-        cols_bf = setup.tile([P, PACK], BF16)
-        nc.scalar.dma_start(out=cols_bf[:], in_=vec.rearrange("(p j) -> p j", j=PACK))
-        nc.vector.tensor_copy(out=ln_cols[:, n * PACK : (n + 1) * PACK], in_=cols_bf[:])
-    return ln_cols
+def load_layer_norm(nc, setup, ln1_w, ln1_b):
+    cols = [setup.tile([P, PACK], BF16, name="cols%d" % n) for n in range(2)]
+    for tile, vec in zip(cols, (ln1_w, ln1_b)):
+        nc.sync.dma_start(out=tile[:], in_=vec.rearrange("(p j) -> p j", j=PACK))
+    return cols
 
 
-def rotary_tables(nc, setup, keep, q_b):
+def load_biases(nc, setup, q_b, v_b):
+    rows_bf = setup.tile([P, P], BF16)
+    nc.gpsimd.memset(rows_bf[:], 0.0)
+    nc.sync.dma_start(
+        out=rows_bf[0:2, :].rearrange("f (h d) -> f h d", h=NH),
+        in_=q_b.rearrange("(h f d) -> f h d", h=NH, f=2),
+    )
+    vrow = setup.tile([P, E], BF16)
+    nc.gpsimd.memset(vrow[:], 0.0)
+    nc.sync.dma_start(out=vrow[0:1, :], in_=v_b.unsqueeze(0))
+    ones = setup.tile([P, P], BF16)
+    nc.gpsimd.memset(ones[:], 1.0)
+    return rows_bf, vrow, ones
+
+
+def spread_biases(nc, setup, keep, psum, ident, rows_bf, vrow, ones):
+    rows = setup.tile([P, P], F32)
+    nc.vector.tensor_copy(out=rows[:], in_=rows_bf[:])
+    cols_ps = psum.tile([P, BANK], F32, tag="xt")
+    nc.tensor.transpose(cols_ps[:, 0:P], rows[:], ident[:])
+    q_bias = keep.tile([P, 2], F32)
+    nc.vector.tensor_copy(out=q_bias[:], in_=cols_ps[:, 0:2])
+    vb_ps = psum.tile([P, BANK], F32, tag="xt")
+    nc.tensor.matmul(vb_ps[:, 0:E], lhsT=ones[:], rhs=vrow[:], start=True, stop=True)
+    v_bias = keep.tile([P, E], F32)
+    nc.vector.tensor_copy(out=v_bias[:], in_=vb_ps[:, 0:E])
+    return q_bias, v_bias
+
+
+def rotary_tables(nc, setup, keep):
     part_i = setup.tile([P, 1], I32)
     nc.gpsimd.iota(part_i[:], pattern=[[0, 1]], base=0, channel_multiplier=1)
-    step_i = setup.tile([P, RUN], I32)
-    nc.gpsimd.iota(step_i[:], pattern=[[1, RUN]], base=0, channel_multiplier=0)
-    row_i = setup.tile([P, 1], I32)
-    nc.vector.tensor_scalar(
-        out=row_i[:], in0=part_i[:], scalar1=1, scalar2=1,
-        op0=ALU.logical_shift_right, op1=ALU.bitwise_and,
-    )
-    half_i = setup.tile([P, 1], I32)
-    nc.vector.tensor_single_scalar(out=half_i[:], in_=part_i[:], scalar=1, op=ALU.bitwise_and)
-    row_f = setup.tile([P, 1], F32)
-    nc.vector.tensor_copy(out=row_f[:], in_=row_i[:])
-    half_f = setup.tile([P, 1], F32)
-    nc.vector.tensor_copy(out=half_f[:], in_=half_i[:])
-    step_f = setup.tile([P, RUN], F32)
-    nc.vector.tensor_copy(out=step_f[:], in_=step_i[:])
-    col0_f = setup.tile([P, 1], F32)
-    nc.vector.tensor_scalar_mul(out=col0_f[:], in0=half_f[:], scalar1=float(RUN))
-    pos = setup.tile([P, 2 * RUN], F32)
-    nc.vector.tensor_scalar(
-        out=pos[:, 0:GROUPS], in0=step_f[:], scalar1=2.0, scalar2=row_f[:, 0:1],
-        op0=ALU.mult, op1=ALU.add,
-    )
-    nc.vector.tensor_scalar_add(out=pos[:, GROUPS:], in0=step_f[:], scalar1=col0_f[:, 0:1])
-    arg = setup.tile([P, 2, 2 * RUN, FREQS], F32)
-    for m in range(FREQS):
-        nc.vector.tensor_scalar_mul(
-            out=arg[:, 1, :, m], in0=pos[:], scalar1=PT / WS * THETA ** (-m / FREQS)
-        )
-    nc.vector.tensor_scalar_add(out=arg[:, 0], in0=arg[:, 1], scalar1=math.pi / 2)
-    largest = (WS - 1) * PT / WS + math.pi / 2
-    for turn in range(math.ceil((largest - math.pi) / (2 * math.pi))):
-        wrap = setup.tile([P, 2, 2 * RUN, FREQS], F32)
+    pos_i = setup.tile([P, WS], I32)
+    nc.gpsimd.iota(pos_i[:], pattern=[[1, WS]], base=0, channel_multiplier=0)
+    pos = setup.tile([P, WS], F32)
+    nc.vector.tensor_copy(out=pos[:], in_=pos_i[:])
+    bits_i = setup.tile([P, 5], I32)
+    for b in range(5):
         nc.vector.tensor_scalar(
-            out=wrap[:], in0=arg[:], scalar1=math.pi, scalar2=-2 * math.pi,
+            out=bits_i[:, b : b + 1], in0=part_i[:], scalar1=b, scalar2=1,
+            op0=ALU.logical_shift_right, op1=ALU.bitwise_and,
+        )
+    bits = setup.tile([P, 5], F32)
+    nc.vector.tensor_copy(out=bits[:], in_=bits_i[:])
+    factors = setup.tile([P, 4], F32)
+    for b in range(4):
+        nc.vector.tensor_scalar(
+            out=factors[:, b : b + 1], in0=bits[:, b + 1 : b + 2],
+            scalar1=THETA ** (-(2**b) / FREQS) - 1.0, scalar2=1.0, op0=ALU.mult, op1=ALU.add,
+        )
+    pairs = setup.tile([P, 2], F32)
+    nc.vector.tensor_tensor(
+        out=pairs[:], in0=factors[:, 0:2], in1=factors[:, 2:4], op=ALU.mult
+    )
+    freq = setup.tile([P, 1], F32)
+    nc.vector.tensor_tensor(
+        out=freq[:], in0=pairs[:, 0:1], in1=pairs[:, 1:2], op=ALU.mult
+    )
+    sign = setup.tile([P, 1], F32)
+    nc.vector.tensor_scalar(
+        out=sign[:], in0=bits[:, 0:1], scalar1=-2.0, scalar2=1.0, op0=ALU.mult, op1=ALU.add
+    )
+    arg = setup.tile([P, 2, WS], F32)
+    for k, offset in enumerate((math.pi / 2, 0.0)):
+        scaled = setup.tile([P, WS], F32, name="scaled%d" % k)
+        nc.vector.tensor_scalar(
+            out=scaled[:], in0=pos[:], scalar1=freq[:, 0:1], scalar2=None, op0=ALU.mult
+        )
+        nc.vector.tensor_scalar(
+            out=arg[:, k, :], in0=scaled[:], scalar1=PT / WS, scalar2=offset,
+            op0=ALU.mult, op1=ALU.add,
+        )
+    largest = (WS - 1) * PT / WS + math.pi / 2
+    wraps = []
+    for turn in range(math.ceil((largest - math.pi) / (2 * math.pi))):
+        wrap = setup.tile([P, 2, WS], F32, name="wrap%d" % turn)
+        nc.vector.tensor_scalar(
+            out=wrap[:], in0=arg[:], scalar1=(2 * turn + 1) * math.pi, scalar2=-2 * math.pi,
             op0=ALU.is_gt, op1=ALU.mult,
         )
+        wraps.append(wrap)
+    for wrap in wraps:
         nc.vector.tensor_tensor(out=arg[:], in0=arg[:], in1=wrap[:], op=ALU.add)
-    cos_sin = setup.tile([P, 2, 2 * RUN, FREQS], F32)
-    nc.scalar.activation(out=cos_sin[:], in_=arg[:], func=ACT.Sin)
-    paired = setup.tile([P, 2, 2 * RUN, HALF], F32)
-    pairs = paired[:].rearrange("p k n (m e) -> p k n m e", e=2)
-    for e in range(2):
-        nc.vector.tensor_copy(out=pairs[:, 0, :, :, e], in_=cos_sin[:, 0])
-    nc.vector.tensor_scalar_mul(out=pairs[:, 1, :, :, 0], in0=cos_sin[:, 1], scalar1=-1.0)
-    nc.vector.tensor_copy(out=pairs[:, 1, :, :, 1], in_=cos_sin[:, 1])
-    table = keep.tile([P, TILES, 2, DH], F32)
-    by_group = table[:].rearrange("p (s c) k d -> p s c k d", c=RUN)
-    shape = [P, GROUPS, RUN, HALF]
+    by_col = keep.tile([P, 2, WS], F32)
+    nc.scalar.activation(out=by_col[:], in_=arg[:], func=ACT.Sin)
+    nc.vector.tensor_scalar(
+        out=by_col[:, 1, :], in0=by_col[:, 1, :], scalar1=sign[:, 0:1], scalar2=None, op0=ALU.mult
+    )
+    by_row = keep.tile([P, 2, (BANDS + 1) * ROWS], F32)
+    nc.vector.tensor_copy(out=by_row[:, :, 0 : BANDS * ROWS], in_=by_col[:, :, 0 : BANDS * ROWS])
+    nc.vector.tensor_copy(
+        out=by_row[:, :, BANDS * ROWS :].rearrange("p k (r h) -> p k r h", h=2),
+        in_=by_col[:, :, BANDS * ROWS :].unsqueeze(3).to_broadcast([P, 2, 2, 2]),
+    )
+    last_col = keep.tile([P, 2, RUN, ROWS], F32)
     for k in range(2):
-        nc.gpsimd.tensor_scalar(
-            out=by_group[:, :, :, k, 0:HALF],
-            in0=paired[:, k, 0:GROUPS].unsqueeze(2).to_broadcast(shape),
-            scalar1=1.0, scalar2=0.0, op0=ALU.mult, op1=ALU.add,
-        )
-        nc.gpsimd.tensor_scalar(
-            out=by_group[:, :, :, k, HALF:DH],
-            in0=paired[:, k, GROUPS:].unsqueeze(1).to_broadcast(shape),
-            scalar1=1.0, scalar2=0.0, op0=ALU.mult, op1=ALU.add,
-        )
-    bias_bf = setup.tile([P, E], BF16)
-    nc.scalar.dma_start(out=bias_bf[:], in_=q_b.partition_broadcast(P))
-    bias = setup.tile([P, 2, NH, DH], F32)
-    nc.vector.tensor_copy(out=bias[:, 0], in_=bias_bf[:].rearrange("p (h d) -> p h d", h=NH))
-    src = bias_bf[:].rearrange("p (h m e) -> p h m e", h=NH, e=2)
-    dst = bias[:, 1].rearrange("p h (m e) -> p h m e", e=2)
-    for e in range(2):
-        nc.vector.tensor_copy(out=dst[:, :, :, e], in_=src[:, :, :, 1 - e])
-    q_rot = keep.tile([P, 2 * RUN, NH, HALF], F32)
-    shape = [P, RUN, NH, HALF]
-    for axis in range(2):
-        n0, d0 = axis * RUN, axis * HALF
-        term0 = setup.tile([P, RUN, NH, HALF], F32)
-        term1 = setup.tile([P, RUN, NH, HALF], F32)
-        for k, term in enumerate((term0, term1)):
-            nc.gpsimd.tensor_tensor(
-                out=term[:],
-                in0=bias[:, k, :, d0 : d0 + HALF].unsqueeze(1).to_broadcast(shape),
-                in1=paired[:, k, n0 : n0 + RUN].unsqueeze(2).to_broadcast(shape),
-                op=ALU.mult,
+        for r in range(2):
+            nc.vector.tensor_copy(
+                out=last_col[:, k, :, 2 * r : 2 * r + 2],
+                in_=by_col[:, k, :].rearrange("p (hf i) -> p i hf", hf=2),
             )
-        nc.gpsimd.tensor_tensor(
-            out=q_rot[:, n0 : n0 + RUN], in0=term0[:], in1=term1[:], op=ALU.add
-        )
-    return table, q_rot
+    return by_row, by_col, last_col
 
 
 def tile_block_pa_t_kernel(
@@ -165,175 +185,340 @@ def tile_block_pa_t_kernel(
         keep = ctx.enter_context(tc.tile_pool(name="keep", bufs=1))
         work = ctx.enter_context(tc.tile_pool(name="work", bufs=2))
         small = ctx.enter_context(tc.tile_pool(name="small", bufs=4))
-        psum_t = ctx.enter_context(tc.psum_pool(name="psum_t", bufs=3))
-        psum_mx = ctx.enter_context(tc.psum_pool(name="psum_mx", bufs=5))
+        stage = ctx.enter_context(tc.tile_pool(name="stage", bufs=3))
+        psum_t = ctx.enter_context(tc.psum_pool(name="psum_t", bufs=2))
+        psum_a = ctx.enter_context(tc.psum_pool(name="psum_a", bufs=1))
+        psum_r = ctx.enter_context(tc.psum_pool(name="psum_r", bufs=2))
 
+        setup = ctx.enter_context(tc.tile_pool(name="setup", bufs=1))
+
+        x_band = x.flatten_outer_dims().rearrange("(bi t) ch -> bi t ch", bi=8)
         x_sb = keep.tile([P, TILES, C], BF16)
-        x_groups = x.flatten_outer_dims().rearrange(
-            "(bi s g c) ch -> s g bi (c ch)", bi=8, s=GROUPS, g=16, c=RUN
-        )
-        for s in range(GROUPS):
+
+        def load(band, first, last):
+            step = WS if band < BANDS else RUN
+            pixels = x_band[:, band * ROWS * 56 : band * ROWS * 56 + 16 * step, :]
+            tile0 = band * WS
             nc.sync.dma_start(
-                out=x_sb[:, s * RUN : (s + 1) * RUN, :].rearrange("p c ch -> p (c ch)"),
-                in_=x_groups[s],
+                out=x_sb[:, tile0 + first : tile0 + last, :].rearrange("p c ch -> p (c ch)"),
+                in_=pixels.rearrange("bi (q c) ch -> q bi c ch", q=16)[:, :, first:last, :].rearrange(
+                    "q bi c ch -> q bi (c ch)"
+                ),
             )
 
-        with tc.tile_pool(name="setup", bufs=1) as setup:
-            ident = setup.tile([P, P], F32)
-            make_identity(nc, ident[:])
-            perm = keep.tile([P, P], F32)
+        ctx.enter_context(tc.manual_schedule())
+        load(0, 0, 2)
+        ln_bf = load_layer_norm(nc, setup, ln1_w, ln1_b)
+        load(0, 2, 4)
+        rows_bf, vrow, ones = load_biases(nc, setup, q_b, v_b)
+        raw = [keep.tile([P, PACK, E], BF16, name="raw%d" % n) for n in range(3)]
+        for tile, w in zip(raw, (q_w, k_w, v_w)):
+            nc.sync.dma_start(out=tile[:], in_=w.rearrange("(p j) e -> p j e", j=PACK))
+        load(0, 4, 8)
+        load(0, 8, WS)
+        load(1, 0, WS)
+        load(2, 0, WS)
+        load(3, 0, RUN)
+
+        zero = setup.tile([P, 1], F32)
+        nc.gpsimd.memset(zero[:], 0.0)
+        dummy = setup.tile([P, 1], F32)
+        nc.scalar.activation(out=dummy[:], in_=zero[:], func=ACT.Sin)
+        eps = keep.tile([P, 1], F32)
+        nc.vector.tensor_scalar_add(out=eps[:], in0=zero[:], scalar1=EPS)
+        ident = keep.tile([P, P], F32)
+        by_row, by_col, last_col = rotary_tables(nc, setup, keep)
+        make_identity(nc, ident[:])
+        perm = keep.tile([P, P], F32)
+        nc.vector.tensor_copy(
+            out=perm[:].rearrange("p (bi j r) -> p bi j r", bi=8, j=4),
+            in_=ident[:].rearrange("p (r j bi) -> p bi j r", r=ROWS, j=4),
+        )
+        ln_cols = keep.tile([P, 2 * PACK], F32)
+        for n, tile in enumerate(ln_bf):
+            nc.vector.tensor_copy(out=ln_cols[:, n * PACK : (n + 1) * PACK], in_=tile[:])
+        swap = keep.tile([P, P], F32)
+        perm_last = keep.tile([P, P], F32)
+
+        def late_constants():
+            for e in range(2):
+                nc.vector.tensor_copy(
+                    out=swap[:].rearrange("p (m e) -> p m e", e=2)[:, :, e],
+                    in_=ident[:].rearrange("p (m e) -> p m e", e=2)[:, :, 1 - e],
+                )
             nc.vector.tensor_copy(
-                out=perm[:].rearrange("p (bi j rl hf) -> p bi j rl hf", bi=8, j=4, rl=2, hf=2),
-                in_=ident[:].rearrange("p (rl j hf bi) -> p bi j rl hf", rl=2, j=4, hf=2, bi=8),
+                out=perm_last[:].rearrange("p (bi j rl hf) -> p bi j rl hf", bi=8, j=4, rl=2),
+                in_=ident[:].rearrange("p (rl j hf bi) -> p bi j rl hf", rl=2, j=4, hf=2),
             )
-            ln_cols = layer_norm_columns(nc, setup, keep, ln1_w, ln1_b)
-            w_codes, w_scales = quantise_weights(nc, setup, keep, q_w, k_w, v_w)
-            table, q_rot = rotary_tables(nc, setup, keep, q_b)
-            vb_bf = setup.tile([P, E], BF16)
-            nc.scalar.dma_start(out=vb_bf[:], in_=v_b.partition_broadcast(P))
-            v_bias = keep.tile([P, NH, DH], F32)
-            nc.vector.tensor_copy(out=v_bias[:], in_=vb_bf[:].rearrange("p (h d) -> p h d", h=NH))
-            eps = keep.tile([P, 1], F32)
-            nc.vector.memset(eps[:], EPS)
+            q_bias, v_bias = spread_biases(nc, setup, keep, psum_t, ident, rows_bf, vrow, ones)
+            bias_col = keep.tile([P, 2, WS], F32)
+            nc.vector.tensor_scalar(
+                out=bias_col[:], in0=by_col[:], scalar1=q_bias[:, 1:2], scalar2=None, op0=ALU.mult
+            )
+            w_codes, w_scales = quantise_weights(nc, setup, keep, raw)
+            return q_bias, v_bias, bias_col, w_codes, w_scales
 
-        stage = ctx.enter_context(tc.tile_pool(name="stage", bufs=2))
-        outs = [
-            o.rearrange("w h (s q c) d -> s h w q (c d)", s=GROUPS, q=4, c=RUN)
-            for o in (out_0, out_1, out_2)
-        ]
-        scale_of, codes_of, stage_of = {}, {}, {}
+        units = units_of_tiles()
+        stats_of, normed_of, planes_of, grouped_of = {}, {}, {}, {}
+        codes_of, acc_of, turned_of, stage_of, turning = {}, {}, {}, {}, {}
 
-        def tiles_of(r):
-            return range(r * ROUND, min((r + 1) * ROUND, TILES))
+        def statistics(r, i):
+            first, n = units[r]
+            if i == 0:
+                six = small.tile([P, 2, 6], F32)
+                mean_var = small.tile([P, 2, 2], F32)
+                stats_of[r] = [six, mean_var]
+            if i < n:
+                nc.vector.bn_stats(out=stats_of[r][0][:, i, :], in_=x_sb[:, first + i, :])
 
-        def statistics(r):
-            n = len(tiles_of(r))
-            six = small.tile([P, ROUND, 6], F32)
-            mean_var = small.tile([P, ROUND, 2], F32)
-            for i, t in enumerate(tiles_of(r)):
-                nc.vector.bn_stats(out=six[:, i, :], in_=x_sb[:, t, :])
+        def finish_statistics(r):
+            n = units[r][1]
+            six, mean_var = stats_of[r]
             for i in range(n):
                 nc.vector.bn_aggr(out=mean_var[:, i, :], in_=six[:, i, :])
-            std = small.tile([P, ROUND], F32)
+
+        def invert_deviation(r):
+            n = units[r][1]
+            mean_var = stats_of[r][1]
+            rstd = small.tile([P, 2], F32)
             nc.scalar.activation(
-                out=std[:, 0:n], in_=mean_var[:, 0:n, 1], func=ACT.Sqrt, bias=eps[:, 0:1], scale=1.0
+                out=rstd[:, 0:n], in_=mean_var[:, 0:n, 1], func=ACT.Abs_reciprocal_sqrt,
+                bias=eps[:, 0:1], scale=1.0,
             )
-            rstd = small.tile([P, ROUND], F32)
-            nc.vector.reciprocal(out=rstd[:, 0:n], in_=std[:, 0:n])
-            shift = small.tile([P, ROUND], F32)
-            nc.vector.scalar_tensor_tensor(
-                out=shift[:, 0:n], in0=mean_var[:, 0:n, 0], scalar=-1.0, in1=rstd[:, 0:n],
-                op0=ALU.mult, op1=ALU.mult,
-            )
-            scale_of[r] = (rstd, shift)
+            stats_of[r] = [mean_var, rstd]
 
-        def normalise_and_transpose(r):
-            n = len(tiles_of(r))
-            rstd, shift = scale_of[r]
-            xn = work.tile([P, ROUND, C], F32)
-            for i, t in enumerate(tiles_of(r)):
-                nc.scalar.activation(
-                    out=xn[:, i, :].rearrange("p (j k) -> p j k", j=PACK),
-                    in_=x_sb[:, t, :].rearrange("p (k j) -> p j k", j=PACK), func=ACT.Identity,
-                    bias=shift[:, i : i + 1], scale=rstd[:, i : i + 1],
+        def negate_mean(r):
+            n = units[r][1]
+            mean_var, rstd = stats_of[r]
+            minus_mean = small.tile([P, 2], F32)
+            nc.gpsimd.tensor_scalar(
+                out=minus_mean[:, 0:n], in0=mean_var[:, 0:n, 0], scalar1=-1.0, scalar2=0.0,
+                op0=ALU.mult, op1=ALU.add,
+            )
+            stats_of[r] = [minus_mean, rstd]
+
+        def normalise(r):
+            first, n = units[r]
+            minus_mean, rstd = stats_of[r]
+            normed = work.tile([P, 2, C], F32)
+            for i in range(n):
+                nc.gpsimd.tensor_scalar(
+                    out=normed[:, i, :].rearrange("p (j k) -> p j k", j=PACK),
+                    in0=x_sb[:, first + i, :].rearrange("p (k j) -> p j k", j=PACK),
+                    scalar1=minus_mean[:, i : i + 1], scalar2=rstd[:, i : i + 1],
+                    op0=ALU.add, op1=ALU.mult,
                 )
-            planes = work.tile([P, PACK, ROUND * P], BF16)
-            for j in range(PACK):
-                xt = psum_t.tile([P, ROUND * P], F32, tag="xt")
-                for i in range(n):
-                    nc.tensor.transpose(
-                        xt[:, i * P : (i + 1) * P], xn[:, i, j * P : (j + 1) * P], perm[:]
+            normed_of[r] = normed
+
+        def transpose_slots(r):
+            first, n = units[r]
+            normed = normed_of[r]
+            planes = work.tile([P, PACK, 2 * P], BF16)
+            order = perm if first < BANDS * WS else perm_last
+            for pair in range(2):
+                xt = psum_t.tile([P, 2, 2 * P], F32, tag="xt")
+                for jj in range(2):
+                    j = 2 * pair + jj
+                    for i in range(n):
+                        nc.tensor.transpose(
+                            xt[:, jj, i * P : (i + 1) * P], normed[:, i, j * P : (j + 1) * P], order[:]
+                        )
+                for jj in range(2):
+                    j = 2 * pair + jj
+                    nc.scalar.activation(
+                        out=planes[:, j, 0 : n * P], in_=xt[:, jj, 0 : n * P], func=ACT.Identity,
+                        bias=ln_cols[:, PACK + j : PACK + j + 1], scale=ln_cols[:, j : j + 1],
                     )
-                nc.scalar.activation(
-                    out=planes[:, j, 0 : n * P], in_=xt[:, 0 : n * P], func=ACT.Identity,
-                    bias=ln_cols[:, PACK + j : PACK + j + 1], scale=ln_cols[:, j : j + 1],
-                )
-            grouped = work.tile([P, ROUND * P, PACK], BF16, align_bytes=64)
-            nc.scalar.copy(
-                out=grouped[:, 0 : n * P, :].rearrange("p (c i) j -> p c j i", i=4),
-                in_=planes[:, :, 0 : n * P].rearrange("p j (c i) -> p c j i", i=4),
-            )
-            codes_of[r] = grouped
+            planes_of[r] = planes
 
-        def project_and_rotate(r):
-            n = len(tiles_of(r))
-            grouped = codes_of[r]
-            codes = work.tile([P, ROUND * P], U32, align_bytes=64)
-            scales = work.tile([P, ROUND * P], U8, align_bytes=64)
-            nc.vector.quantize_mx(
-                out=codes[:, 0 : n * P].bitcast(FP8X4),
-                scales=scales[:, 0 : n * P],
-                in_=grouped[:, 0 : n * P, :].rearrange("p t j -> p (t j)"),
+        def interleave(r):
+            n = units[r][1]
+            grouped = work.tile([P, 2 * P, PACK], BF16, align_bytes=64)
+            nc.gpsimd.tensor_scalar(
+                out=grouped[:, 0 : n * P, :],
+                in0=planes_of[r][:, :, 0 : n * P].rearrange("p j c -> p c j"),
+                scalar1=1.0, scalar2=0.0, op0=ALU.mult, op1=ALU.add,
             )
-            for i, t in enumerate(tiles_of(r)):
-                s, c = divmod(t, RUN)
-                if c == 0:
-                    qk_new = stage.tile([P, 2, 2, NH, RUN, DH], F32, name="qk_stage")
-                    v_new = stage.tile([P, NH, RUN, DH], F32, name="v_stage")
-                    stage_of[s] = (qk_new, v_new)
-                qk_stage, v_stage = stage_of[s]
-                tokens = slice(i * P, (i + 1) * P)
-                for n_out in range(2):
-                    acc = psum_mx.tile([P, 2 * E], F32, tag="mx")
-                    cols = slice(n_out * 2 * E, (n_out + 1) * 2 * E)
+            grouped_of[r] = grouped
+
+        def quantise(r):
+            n = units[r][1]
+            codes = work.tile([P, 2 * P], U32, align_bytes=64)
+            scales = work.tile([P, 2 * P], U8, align_bytes=64)
+            nc.vector.quantize_mx(
+                out=codes[:, 0 : n * P].bitcast(FP8X4), scales=scales[:, 0 : n * P],
+                in_=grouped_of[r][:, 0 : n * P, :].rearrange("p t j -> p (t j)"),
+            )
+            codes_of[r] = (codes, scales)
+
+        def project(r):
+            n = units[r][1]
+            codes, scales = codes_of[r]
+            acc_a = psum_a.tile([P, 2, 2 * P], F32)
+            acc_b = psum_a.tile([P, 2, 2 * P], F32)
+            acc_v = psum_a.tile([P, 2, E], F32)
+            for f, acc in enumerate((acc_a, acc_b)):
+                for m in range(2):
+                    weights = slice((2 * m + f) * P, (2 * m + f + 1) * P)
                     nc.tensor.matmul_mx(
-                        out=acc[:],
-                        lhsT=codes[:, tokens].bitcast(FP8X4), lhsT_scale=scales[:, tokens],
-                        rhs=w_codes[:, cols].bitcast(FP8X4), rhs_scale=w_scales[:, cols],
+                        out=acc[:, m, 0 : n * P],
+                        lhsT=w_codes[:, weights].bitcast(FP8X4), lhsT_scale=w_scales[:, weights],
+                        rhs=codes[:, 0 : n * P].bitcast(FP8X4), rhs_scale=scales[:, 0 : n * P],
                         start=True, stop=True,
                     )
-                    nc.vector.tensor_tensor(
-                        out=qk_stage[:, n_out, :, :, c, :],
-                        in0=acc[:].rearrange("p (k h d) -> p k h d", k=2, h=NH),
-                        in1=table[:, t].unsqueeze(2).to_broadcast([P, 2, NH, DH]),
-                        op=ALU.mult,
-                    )
-                acc_v = psum_mx.tile([P, 2 * E], F32, tag="mx")
-                cols = slice(4 * E, 5 * E)
+            weights = slice(2 * E, 3 * E)
+            for i in range(n):
+                tokens = slice(i * P, (i + 1) * P)
                 nc.tensor.matmul_mx(
-                    out=acc_v[:, 0:E],
+                    out=acc_v[:, i, :],
                     lhsT=codes[:, tokens].bitcast(FP8X4), lhsT_scale=scales[:, tokens],
-                    rhs=w_codes[:, cols].bitcast(FP8X4), rhs_scale=w_scales[:, cols],
+                    rhs=w_codes[:, weights].bitcast(FP8X4), rhs_scale=w_scales[:, weights],
                     start=True, stop=True,
                 )
+            acc_of[r] = (acc_a, acc_b, acc_v)
+            turned_a0 = work.tile([P, 2, 2 * P], F32)
+            turned_a1 = work.tile([P, 2, 2 * P], F32)
+            turned_b0 = work.tile([P, 2, 2 * P], F32)
+            turned_b1 = work.tile([P, 2, 2 * P], F32)
+            turned_of[r] = ((turned_a0, turned_a1), (turned_b0, turned_b1))
+
+        def times_table(r, f, m, tokens, table):
+            for k in range(2):
+                shape = [P, (tokens.stop - tokens.start) // ROWS, ROWS]
+                spread = table[k].unsqueeze(1).to_broadcast(shape)
+                source = acc_of[r][f][:, m, tokens].rearrange("p (w r) -> p w r", r=ROWS)
+                target = turned_of[r][f][k][:, m, tokens].rearrange("p (w r) -> p w r", r=ROWS)
+                if m == 0:
+                    nc.vector.scalar_tensor_tensor(
+                        out=target, in0=source, scalar=q_bias[:, f : f + 1], in1=spread,
+                        op0=ALU.add, op1=ALU.mult,
+                    )
+                else:
+                    nc.vector.tensor_tensor(out=target, in0=source, in1=spread, op=ALU.mult)
+
+        def rotate_rows(r, m):
+            first, n = units[r]
+            band = first // WS
+            table = [by_row[:, k, band * ROWS : (band + 1) * ROWS] for k in range(2)]
+            times_table(r, 0, m, slice(0, n * P), table)
+
+        def rotate_columns(r, i):
+            first, n = units[r]
+            if i >= n:
+                return
+            tokens = slice(i * P, (i + 1) * P)
+            band, c = divmod(first + i, WS)
+            for m in range(2):
+                if band == BANDS:
+                    times_table(r, 1, m, tokens, [last_col[:, k, c, :] for k in range(2)])
+                    continue
+                for k in range(2):
+                    nc.scalar.activation(
+                        out=turned_of[r][1][k][:, m, tokens], in_=acc_of[r][1][:, m, tokens],
+                        func=ACT.Identity, scale=by_col[:, k, c : c + 1],
+                        bias=bias_col[:, k, c : c + 1] if m == 0 else 0.0,
+                    )
+
+        def staged(t):
+            run, c = divmod(t, RUN)
+            if run not in stage_of:
+                qk_new = stage.tile([P, 2, NH, RUN, DH], F32, name="qk_stage")
+                v_new = stage.tile([P, NH, RUN, DH], F32, name="v_stage")
+                stage_of[run] = (qk_new, v_new)
+            return stage_of[run], c
+
+        def finish_values(r):
+            first, n = units[r]
+            acc_v = acc_of[r][2]
+            i = 0
+            while i < n:
+                tiles, c = staged(first + i)
+                count = min(n - i, RUN - c)
                 nc.vector.tensor_tensor(
-                    out=v_stage[:, :, c, :],
-                    in0=acc_v[:, 0:E].rearrange("p (h d) -> p h d", h=NH),
-                    in1=v_bias[:], op=ALU.add,
+                    out=tiles[1][:, :, c : c + count, :].rearrange("p h c d -> p c h d"),
+                    in0=acc_v[:, i : i + count, :].rearrange("p c (h d) -> p c h d", h=NH),
+                    in1=v_bias[:].rearrange("p (h d) -> p h d", h=NH).unsqueeze(1).to_broadcast(
+                        [P, count, NH, DH]
+                    ),
+                    op=ALU.add,
                 )
-                if c == RUN - 1:
-                    finish_group(s)
+                i += count
+                if c + count == RUN:
+                    store((first + i - 1) // RUN, 2)
 
-        def finish_group(s):
-            qk_stage, v_stage = stage_of[s]
+        def turn_back(r, i):
+            if i >= units[r][1]:
+                return
+            tokens = slice(i * P, (i + 1) * P)
+            out_ps = psum_r.tile([P, 2, NH, DH], F32, tag="turn")
+            for f in range(2):
+                for m in range(2):
+                    target = out_ps[:, m, :, f * HALF : (f + 1) * HALF]
+                    for k, order in enumerate((ident, swap)):
+                        nc.tensor.matmul(
+                            target, lhsT=turned_of[r][f][k][:, m, tokens],
+                            rhs=order[:].rearrange("p (h d) -> p h d", h=NH),
+                            start=k == 0, stop=k == 1, is_transpose=True,
+                        )
+            turning[r, i] = out_ps
+
+        def leave(r, i):
+            if i >= units[r][1]:
+                return
+            t = units[r][0] + i
+            tiles, c = staged(t)
+            nc.scalar.copy(out=tiles[0][:, :, :, c, :], in_=turning[r, i][:])
+            if c == RUN - 1:
+                store(t // RUN, 0)
+                store(t // RUN, 1)
+
+        def store(run, n_out):
+            qk_stage, v_stage = stage_of[run]
+            band, part = divmod(run, 2)
+            o = (out_0, out_1, out_2)[n_out]
+            if band < BANDS:
+                rows = o.rearrange("w h (r c) d -> h w r c d", c=WS)[
+                    :, :, band * ROWS : (band + 1) * ROWS, part * RUN : (part + 1) * RUN, :
+                ]
+            else:
+                rows = o.rearrange("w h (r c) d -> h w r c d", c=RUN)[:, :, 2 * BANDS * ROWS :]
             for h in range(NH):
+                src = v_stage[:, h] if n_out == 2 else qk_stage[:, n_out, h]
                 nc.sync.dma_start(
-                    out=outs[2][s, h], in_=v_stage[:, h].rearrange("p c d -> p (c d)")
+                    out=rows[h].rearrange("w r c d -> w r (c d)"),
+                    in_=src.rearrange("p c d -> p (c d)"),
                 )
-            for n_out in range(2):
-                done = qk_stage[:, n_out, 0]
-                nc.gpsimd.tensor_tensor(
-                    out=done, in0=done, in1=qk_stage[:, n_out, 1], op=ALU.add
-                )
-                if n_out == 0:
-                    shape = [P, NH, RUN, HALF]
-                    nc.gpsimd.tensor_tensor(
-                        out=done[:, :, :, 0:HALF], in0=done[:, :, :, 0:HALF],
-                        in1=q_rot[:, s].unsqueeze(2).to_broadcast(shape), op=ALU.add,
-                    )
-                    nc.gpsimd.tensor_tensor(
-                        out=done[:, :, :, HALF:DH], in0=done[:, :, :, HALF:DH],
-                        in1=q_rot[:, GROUPS:].rearrange("p c h d -> p h c d"), op=ALU.add,
-                    )
-                for h in range(NH):
-                    nc.sync.dma_start(
-                        out=outs[n_out][s, h], in_=done[:, h].rearrange("p c d -> p (c d)")
-                    )
 
-        for step in range(ROUNDS + 2):
-            if step < ROUNDS:
-                statistics(step)
-            if 1 <= step <= ROUNDS:
-                normalise_and_transpose(step - 1)
-            if step >= 2:
-                project_and_rotate(step - 2)
+        last = len(units)
+        for s in range(last + 4):
+            stats, norm, lace, proj, turn = (
+                s - lag if 0 <= s - lag < last else None for lag in range(5)
+            )
+            if s == 2:
+                q_bias, v_bias, bias_col, w_codes, w_scales = late_constants()
+            if proj is not None:
+                quantise(proj)
+                project(proj)
+            if stats is not None:
+                statistics(stats, 0)
+                statistics(stats, 1)
+                finish_statistics(stats)
+            if proj is not None:
+                rotate_rows(proj, 0)
+                rotate_columns(proj, 0)
+                rotate_rows(proj, 1)
+                rotate_columns(proj, 1)
+                finish_values(proj)
+            if turn is not None:
+                for i in range(2):
+                    turn_back(turn, i)
+                    leave(turn, i)
+            if stats is not None:
+                invert_deviation(stats)
+            if norm is not None:
+                normalise(norm)
+                transpose_slots(norm)
+            if lace is not None:
+                interleave(lace)
+            if stats is not None:
+                negate_mean(stats)

@@ -26,6 +26,7 @@ THETA = 10000.0
 EPS = 1e-6
 ROWS = 4
 BANDS = 3
+BY_MATMUL = (1,)
 RUN = 7
 TILES = BANDS * WS + RUN
 BANK = 512
@@ -258,6 +259,18 @@ def tile_block_pa_t_kernel(
             w_codes, w_scales = quantise_weights(nc, setup, keep, raw)
             return q_bias, v_bias, bias_col, w_codes, w_scales
 
+        turns = keep.tile([P, WS, P], F32)
+
+        def make_turn(c):
+            sines = small.tile([P, P], F32)
+            nc.scalar.activation(
+                out=sines[:], in_=swap[:], func=ACT.Copy, scale=by_col[:, 1, c : c + 1]
+            )
+            nc.vector.scalar_tensor_tensor(
+                out=turns[:, c, :], in0=ident[:], scalar=by_col[:, 0, c : c + 1], in1=sines[:],
+                op0=ALU.mult, op1=ALU.add,
+            )
+
         units = units_of_tiles()
         stats_of, normed_of, planes_of, grouped_of = {}, {}, {}, {}
         codes_of, acc_of, turned_of, stage_of, turning = {}, {}, {}, {}, {}
@@ -409,6 +422,13 @@ def tile_block_pa_t_kernel(
             tokens = slice(i * P, (i + 1) * P)
             band, c = divmod(first + i, WS)
             for m in range(2):
+                if band < BANDS and m in BY_MATMUL:
+                    if i == 0:
+                        nc.scalar.activation(
+                            out=turned_of[r][1][0][:, m, 0 : n * P], in_=acc_of[r][1][:, m, 0 : n * P],
+                            func=ACT.Identity, bias=q_bias[:, 1:2] if m == 0 else 0.0, scale=1.0,
+                        )
+                    continue
                 if band == BANDS:
                     times_table(r, 1, m, tokens, [last_col[:, k, c, :] for k in range(2)])
                     continue
@@ -454,6 +474,14 @@ def tile_block_pa_t_kernel(
             for f in range(2):
                 for m in range(2):
                     target = out_ps[:, m, :, f * HALF : (f + 1) * HALF]
+                    band, c = divmod(units[r][0] + i, WS)
+                    if f == 1 and m in BY_MATMUL and band < BANDS:
+                        nc.tensor.matmul(
+                            target, lhsT=turned_of[r][f][0][:, m, tokens],
+                            rhs=turns[:, c, :].rearrange("p (h d) -> p h d", h=NH),
+                            start=True, stop=True,
+                        )
+                        continue
                     for k, order in enumerate((ident, swap)):
                         nc.tensor.matmul(
                             target, lhsT=turned_of[r][f][k][:, m, tokens],
@@ -499,6 +527,9 @@ def tile_block_pa_t_kernel(
             if proj is not None:
                 quantise(proj)
                 project(proj)
+                if proj < WS // 2:
+                    make_turn(2 * proj)
+                    make_turn(2 * proj + 1)
             if stats is not None:
                 statistics(stats, 0)
                 statistics(stats, 1)

@@ -261,14 +261,19 @@ def tile_block_pa_t_kernel(
 
         turns = keep.tile([P, WS, P], F32)
 
-        def make_turn(c):
+        sines_of = {}
+
+        def make_sines(c):
             sines = small.tile([P, P], F32)
             nc.scalar.activation(
                 out=sines[:], in_=swap[:], func=ACT.Copy, scale=by_col[:, 1, c : c + 1]
             )
+            sines_of[c] = sines
+
+        def make_turn(c):
             nc.vector.scalar_tensor_tensor(
-                out=turns[:, c, :], in0=ident[:], scalar=by_col[:, 0, c : c + 1], in1=sines[:],
-                op0=ALU.mult, op1=ALU.add,
+                out=turns[:, c, :], in0=ident[:], scalar=by_col[:, 0, c : c + 1],
+                in1=sines_of[c][:], op0=ALU.mult, op1=ALU.add,
             )
 
         units = units_of_tiles()
@@ -347,11 +352,13 @@ def tile_block_pa_t_kernel(
         def interleave(r):
             n = units[r][1]
             grouped = work.tile([P, 2 * P, PACK], BF16, align_bytes=64)
-            nc.gpsimd.tensor_scalar(
-                out=grouped[:, 0 : n * P, :],
-                in0=planes_of[r][:, :, 0 : n * P].rearrange("p j c -> p c j"),
-                scalar1=1.0, scalar2=0.0, op0=ALU.mult, op1=ALU.add,
-            )
+            for i in range(n):
+                tokens = slice(i * P, (i + 1) * P)
+                nc.gpsimd.tensor_scalar(
+                    out=grouped[:, tokens, :],
+                    in0=planes_of[r][:, :, tokens].rearrange("p j c -> p c j"),
+                    scalar1=1.0, scalar2=0.0, op0=ALU.mult, op1=ALU.add,
+                )
             grouped_of[r] = grouped
 
         def quantise(r):
@@ -527,9 +534,6 @@ def tile_block_pa_t_kernel(
             if proj is not None:
                 quantise(proj)
                 project(proj)
-                if proj < WS // 2:
-                    make_turn(2 * proj)
-                    make_turn(2 * proj + 1)
             if stats is not None:
                 statistics(stats, 0)
                 statistics(stats, 1)
@@ -540,6 +544,9 @@ def tile_block_pa_t_kernel(
                 rotate_rows(proj, 1)
                 rotate_columns(proj, 1)
                 finish_values(proj)
+                if proj < WS // 2:
+                    make_turn(2 * proj)
+                    make_turn(2 * proj + 1)
             if turn is not None:
                 for i in range(2):
                     turn_back(turn, i)
@@ -551,5 +558,8 @@ def tile_block_pa_t_kernel(
                 transpose_slots(norm)
             if lace is not None:
                 interleave(lace)
+                if lace < WS // 2:
+                    make_sines(2 * lace)
+                    make_sines(2 * lace + 1)
             if stats is not None:
                 negate_mean(stats)

@@ -26,7 +26,7 @@ THETA = 10000.0
 EPS = 1e-6
 ROWS = 4
 BANDS = 3
-BY_MATMUL = (1,)
+BY_MATMUL = (0, 1)
 RUN = 7
 TILES = BANDS * WS + RUN
 BANK = 512

@@ -303,21 +303,21 @@ def tile_block_pa_t_kernel(
                 out=rstd[:, 0:n], in_=mean_var[:, 0:n, 1], func=ACT.Abs_reciprocal_sqrt,
                 bias=eps[:, 0:1], scale=1.0,
             )
-            stats_of[r] = [mean_var, rstd]
+            stats_of[r].append(rstd)
 
         def negate_mean(r):
             n = units[r][1]
-            mean_var, rstd = stats_of[r]
+            mean_var = stats_of[r][1]
             minus_mean = small.tile([P, 2], F32)
             nc.gpsimd.tensor_scalar(
                 out=minus_mean[:, 0:n], in0=mean_var[:, 0:n, 0], scalar1=-1.0, scalar2=0.0,
                 op0=ALU.mult, op1=ALU.add,
             )
-            stats_of[r] = [minus_mean, rstd]
+            stats_of[r].append(minus_mean)
 
         def normalise(r):
             first, n = units[r]
-            minus_mean, rstd = stats_of[r]
+            minus_mean, rstd = stats_of[r][2:4]
             normed = work.tile([P, 2, C], F32)
             for i in range(n):
                 nc.gpsimd.tensor_scalar(
@@ -354,11 +354,17 @@ def tile_block_pa_t_kernel(
             grouped = work.tile([P, 2 * P, PACK], BF16, align_bytes=64)
             for i in range(n):
                 tokens = slice(i * P, (i + 1) * P)
-                nc.gpsimd.tensor_scalar(
-                    out=grouped[:, tokens, :],
-                    in0=planes_of[r][:, :, tokens].rearrange("p j c -> p c j"),
-                    scalar1=1.0, scalar2=0.0, op0=ALU.mult, op1=ALU.add,
-                )
+                if i == 1:
+                    nc.scalar.copy(
+                        out=grouped[:, tokens, :].rearrange("p (c i) j -> p c j i", i=4),
+                        in_=planes_of[r][:, :, tokens].rearrange("p j (c i) -> p c j i", i=4),
+                    )
+                else:
+                    nc.gpsimd.tensor_scalar(
+                        out=grouped[:, tokens, :],
+                        in0=planes_of[r][:, :, tokens].rearrange("p j c -> p c j"),
+                        scalar1=1.0, scalar2=0.0, op0=ALU.mult, op1=ALU.add,
+                    )
             grouped_of[r] = grouped
 
         def quantise(r):
@@ -534,10 +540,15 @@ def tile_block_pa_t_kernel(
             if proj is not None:
                 quantise(proj)
                 project(proj)
+            if norm is not None:
+                normalise(norm)
+            if lace is not None:
+                interleave(lace)
             if stats is not None:
                 statistics(stats, 0)
                 statistics(stats, 1)
                 finish_statistics(stats)
+                negate_mean(stats)
             if proj is not None:
                 rotate_rows(proj, 0)
                 rotate_columns(proj, 0)
@@ -554,12 +565,7 @@ def tile_block_pa_t_kernel(
             if stats is not None:
                 invert_deviation(stats)
             if norm is not None:
-                normalise(norm)
                 transpose_slots(norm)
-            if lace is not None:
-                interleave(lace)
-                if lace < WS // 2:
-                    make_sines(2 * lace)
-                    make_sines(2 * lace + 1)
-            if stats is not None:
-                negate_mean(stats)
+            if lace is not None and lace < WS // 2:
+                make_sines(2 * lace)
+                make_sines(2 * lace + 1)

@@ -26,7 +26,6 @@ THETA = 10000.0
 EPS = 1e-6
 ROWS = 4
 BANDS = 3
-BY_MATMUL = (0, 1)
 RUN = 7
 TILES = BANDS * WS + RUN
 BANK = 512
@@ -36,28 +35,28 @@ FLOPS = 2 * 6272 * C * 3 * E
 
 def units_of_tiles():
     units = [(2 * u, 2) for u in range(BANDS * WS // 2)]
-    for i in range(0, RUN, 2):
-        units.append((BANDS * WS + i, min(2, RUN - i)))
-    return units
+    last_group = [(BANDS * WS + i, min(2, RUN - i)) for i in range(0, RUN, 2)]
+    end = [(BANDS * WS - 2, 1), (BANDS * WS - 1, 1)]
+    return units[: WS // 2] + last_group + units[WS // 2 : -1] + end
 
 
-def quantise_weights(nc, setup, keep, raws):
+def group_weights(nc, setup, raws):
+    grouped = setup.tile([P, 3 * E, PACK], BF16, align_bytes=64)
+    for n in range(2):
+        src = raws[n][:].rearrange("p j (h f d) -> p f h d j", h=NH, f=2)
+        for f in range(2):
+            first = n * E + f * P
+            nc.scalar.copy(
+                out=grouped[:, first : first + P, :].rearrange("p (h d) j -> p h d j", h=NH),
+                in_=src[:, f],
+            )
+    nc.vector.tensor_copy(out=grouped[:, 2 * E :, :], in_=raws[2][:].rearrange("p j e -> p e j"))
+    return grouped
+
+
+def quantise_weights(nc, keep, grouped):
     w_codes = keep.tile([P, 3 * E], U32, align_bytes=64)
     w_scales = keep.tile([P, 3 * E], U8, align_bytes=64)
-    grouped = setup.tile([P, 3 * E, PACK], BF16, align_bytes=64)
-    for n, raw in enumerate(raws):
-        if n < 2:
-            src = raw[:].rearrange("p j (h f d) -> p f h d j", h=NH, f=2)
-            for f in range(2):
-                first = n * E + f * P
-                nc.vector.tensor_copy(
-                    out=grouped[:, first : first + P, :].rearrange("p (h d) j -> p h d j", h=NH),
-                    in_=src[:, f],
-                )
-        else:
-            nc.vector.tensor_copy(
-                out=grouped[:, 2 * E :, :], in_=raw[:].rearrange("p j e -> p e j")
-            )
     for first, last in ((0, 2 * E), (2 * E, 3 * E)):
         nc.vector.quantize_mx(
             out=w_codes[:, first:last].bitcast(FP8X4),
@@ -76,38 +75,31 @@ def load_layer_norm(nc, setup, ln1_w, ln1_b):
 
 def load_biases(nc, setup, q_b, v_b):
     rows_bf = setup.tile([P, P], BF16)
-    nc.gpsimd.memset(rows_bf[:], 0.0)
+    nc.vector.memset(rows_bf[:], 0.0)
     nc.sync.dma_start(
         out=rows_bf[0:2, :].rearrange("f (h d) -> f h d", h=NH),
         in_=q_b.rearrange("(h f d) -> f h d", h=NH, f=2),
     )
     vrow = setup.tile([P, E], BF16)
-    nc.gpsimd.memset(vrow[:], 0.0)
+    nc.vector.memset(vrow[:], 0.0)
     nc.sync.dma_start(out=vrow[0:1, :], in_=v_b.unsqueeze(0))
     ones = setup.tile([P, P], BF16)
-    nc.gpsimd.memset(ones[:], 1.0)
     return rows_bf, vrow, ones
 
 
-def spread_biases(nc, setup, keep, psum, ident, rows_bf, vrow, ones):
-    rows = setup.tile([P, P], F32)
-    nc.vector.tensor_copy(out=rows[:], in_=rows_bf[:])
+def spread_biases(nc, keep, psum, ident, rows, vrow, ones):
     cols_ps = psum.tile([P, BANK], F32, tag="xt")
     nc.tensor.transpose(cols_ps[:, 0:P], rows[:], ident[:])
-    q_bias = keep.tile([P, 2], F32)
-    nc.vector.tensor_copy(out=q_bias[:], in_=cols_ps[:, 0:2])
     vb_ps = psum.tile([P, BANK], F32, tag="xt")
     nc.tensor.matmul(vb_ps[:, 0:E], lhsT=ones[:], rhs=vrow[:], start=True, stop=True)
+    q_bias = keep.tile([P, 2], F32)
+    nc.vector.tensor_copy(out=q_bias[:], in_=cols_ps[:, 0:2])
     v_bias = keep.tile([P, E], F32)
     nc.vector.tensor_copy(out=v_bias[:], in_=vb_ps[:, 0:E])
     return q_bias, v_bias
 
 
-def rotary_tables(nc, setup, keep):
-    part_i = setup.tile([P, 1], I32)
-    nc.gpsimd.iota(part_i[:], pattern=[[0, 1]], base=0, channel_multiplier=1)
-    pos_i = setup.tile([P, WS], I32)
-    nc.gpsimd.iota(pos_i[:], pattern=[[1, WS]], base=0, channel_multiplier=0)
+def rotary_angles(nc, setup, part_i, pos_i):
     pos = setup.tile([P, WS], F32)
     nc.vector.tensor_copy(out=pos[:], in_=pos_i[:])
     bits_i = setup.tile([P, 5], I32)
@@ -129,8 +121,9 @@ def rotary_tables(nc, setup, keep):
         out=pairs[:], in0=factors[:, 0:2], in1=factors[:, 2:4], op=ALU.mult
     )
     freq = setup.tile([P, 1], F32)
-    nc.vector.tensor_tensor(
-        out=freq[:], in0=pairs[:, 0:1], in1=pairs[:, 1:2], op=ALU.mult
+    nc.vector.scalar_tensor_tensor(
+        out=freq[:], in0=pairs[:, 0:1], scalar=PT / WS, in1=pairs[:, 1:2],
+        op0=ALU.mult, op1=ALU.mult,
     )
     sign = setup.tile([P, 1], F32)
     nc.vector.tensor_scalar(
@@ -138,12 +131,8 @@ def rotary_tables(nc, setup, keep):
     )
     arg = setup.tile([P, 2, WS], F32)
     for k, offset in enumerate((math.pi / 2, 0.0)):
-        scaled = setup.tile([P, WS], F32, name="scaled%d" % k)
         nc.vector.tensor_scalar(
-            out=scaled[:], in0=pos[:], scalar1=freq[:, 0:1], scalar2=None, op0=ALU.mult
-        )
-        nc.vector.tensor_scalar(
-            out=arg[:, k, :], in0=scaled[:], scalar1=PT / WS, scalar2=offset,
+            out=arg[:, k, :], in0=pos[:], scalar1=freq[:, 0:1], scalar2=offset,
             op0=ALU.mult, op1=ALU.add,
         )
     largest = (WS - 1) * PT / WS + math.pi / 2
@@ -157,8 +146,10 @@ def rotary_tables(nc, setup, keep):
         wraps.append(wrap)
     for wrap in wraps:
         nc.vector.tensor_tensor(out=arg[:], in0=arg[:], in1=wrap[:], op=ALU.add)
-    by_col = keep.tile([P, 2, WS], F32)
-    nc.scalar.activation(out=by_col[:], in_=arg[:], func=ACT.Sin)
+    return arg, sign
+
+
+def rotary_tables(nc, keep, by_col, sign):
     nc.vector.tensor_scalar(
         out=by_col[:, 1, :], in0=by_col[:, 1, :], scalar1=sign[:, 0:1], scalar2=None, op0=ALU.mult
     )
@@ -175,7 +166,7 @@ def rotary_tables(nc, setup, keep):
                 out=last_col[:, k, :, 2 * r : 2 * r + 2],
                 in_=by_col[:, k, :].rearrange("p (hf i) -> p i hf", hf=2),
             )
-    return by_row, by_col, last_col
+    return by_row, last_col
 
 
 def tile_block_pa_t_kernel(
@@ -211,25 +202,33 @@ def tile_block_pa_t_kernel(
         load(0, 0, 2)
         ln_bf = load_layer_norm(nc, setup, ln1_w, ln1_b)
         load(0, 2, 4)
+        zero = setup.tile([P, 1], F32)
+        nc.vector.memset(zero[:], 0.0)
         rows_bf, vrow, ones = load_biases(nc, setup, q_b, v_b)
         raw = [keep.tile([P, PACK, E], BF16, name="raw%d" % n) for n in range(3)]
         for tile, w in zip(raw, (q_w, k_w, v_w)):
             nc.sync.dma_start(out=tile[:], in_=w.rearrange("(p j) e -> p j e", j=PACK))
         load(0, 4, 8)
         load(0, 8, WS)
+        load(3, 0, RUN)
         load(1, 0, WS)
         load(2, 0, WS)
-        load(3, 0, RUN)
 
-        zero = setup.tile([P, 1], F32)
-        nc.gpsimd.memset(zero[:], 0.0)
         dummy = setup.tile([P, 1], F32)
         nc.scalar.activation(out=dummy[:], in_=zero[:], func=ACT.Sin)
         eps = keep.tile([P, 1], F32)
         nc.vector.tensor_scalar_add(out=eps[:], in0=zero[:], scalar1=EPS)
+        part_i = setup.tile([P, 1], I32)
+        nc.gpsimd.iota(part_i[:], pattern=[[0, 1]], base=0, channel_multiplier=1)
+        pos_i = setup.tile([P, WS], I32)
+        nc.gpsimd.iota(pos_i[:], pattern=[[1, WS]], base=0, channel_multiplier=0)
         ident = keep.tile([P, P], F32)
-        by_row, by_col, last_col = rotary_tables(nc, setup, keep)
         make_identity(nc, ident[:])
+        nc.gpsimd.memset(ones[:], 1.0)
+        arg, sign = rotary_angles(nc, setup, part_i, pos_i)
+        by_col = keep.tile([P, 2, WS], F32)
+        nc.scalar.activation(out=by_col[:], in_=arg[:], func=ACT.Sin)
+        nc.scalar.activation(out=dummy[:], in_=eps[:], func=ACT.Abs_reciprocal_sqrt)
         perm = keep.tile([P, P], F32)
         nc.vector.tensor_copy(
             out=perm[:].rearrange("p (bi j r) -> p bi j r", bi=8, j=4),
@@ -238,10 +237,12 @@ def tile_block_pa_t_kernel(
         ln_cols = keep.tile([P, 2 * PACK], F32)
         for n, tile in enumerate(ln_bf):
             nc.vector.tensor_copy(out=ln_cols[:, n * PACK : (n + 1) * PACK], in_=tile[:])
+        bias_rows = setup.tile([P, P], F32)
+        nc.vector.tensor_copy(out=bias_rows[:], in_=rows_bf[:])
         swap = keep.tile([P, P], F32)
         perm_last = keep.tile([P, P], F32)
 
-        def late_constants():
+        def permutations():
             for e in range(2):
                 nc.vector.tensor_copy(
                     out=swap[:].rearrange("p (m e) -> p m e", e=2)[:, :, e],
@@ -251,13 +252,6 @@ def tile_block_pa_t_kernel(
                 out=perm_last[:].rearrange("p (bi j rl hf) -> p bi j rl hf", bi=8, j=4, rl=2),
                 in_=ident[:].rearrange("p (rl j hf bi) -> p bi j rl hf", rl=2, j=4, hf=2),
             )
-            q_bias, v_bias = spread_biases(nc, setup, keep, psum_t, ident, rows_bf, vrow, ones)
-            bias_col = keep.tile([P, 2, WS], F32)
-            nc.vector.tensor_scalar(
-                out=bias_col[:], in0=by_col[:], scalar1=q_bias[:, 1:2], scalar2=None, op0=ALU.mult
-            )
-            w_codes, w_scales = quantise_weights(nc, setup, keep, raw)
-            return q_bias, v_bias, bias_col, w_codes, w_scales
 
         turns = keep.tile([P, WS, P], F32)
 
@@ -428,29 +422,23 @@ def tile_block_pa_t_kernel(
             table = [by_row[:, k, band * ROWS : (band + 1) * ROWS] for k in range(2)]
             times_table(r, 0, m, slice(0, n * P), table)
 
-        def rotate_columns(r, i):
+        def rotate_columns(r):
             first, n = units[r]
-            if i >= n:
-                return
-            tokens = slice(i * P, (i + 1) * P)
-            band, c = divmod(first + i, WS)
-            for m in range(2):
-                if band < BANDS and m in BY_MATMUL:
-                    if i == 0:
-                        nc.scalar.activation(
-                            out=turned_of[r][1][0][:, m, 0 : n * P], in_=acc_of[r][1][:, m, 0 : n * P],
-                            func=ACT.Identity, bias=q_bias[:, 1:2] if m == 0 else 0.0, scale=1.0,
+            acc = acc_of[r][1]
+            if first >= BANDS * WS:
+                for i in range(n):
+                    c = first - BANDS * WS + i
+                    for m in range(2):
+                        times_table(
+                            r, 1, m, slice(i * P, (i + 1) * P), [last_col[:, k, c, :] for k in range(2)]
                         )
-                    continue
-                if band == BANDS:
-                    times_table(r, 1, m, tokens, [last_col[:, k, c, :] for k in range(2)])
-                    continue
-                for k in range(2):
-                    nc.scalar.activation(
-                        out=turned_of[r][1][k][:, m, tokens], in_=acc_of[r][1][:, m, tokens],
-                        func=ACT.Identity, scale=by_col[:, k, c : c + 1],
-                        bias=bias_col[:, k, c : c + 1] if m == 0 else 0.0,
-                    )
+                return
+            target = turned_of[r][1][0]
+            nc.scalar.activation(
+                out=target[:, 0, 0 : n * P], in_=acc[:, 0, 0 : n * P], func=ACT.Identity,
+                bias=q_bias[:, 1:2], scale=1.0,
+            )
+            nc.scalar.copy(out=target[:, 1, 0 : n * P], in_=acc[:, 1, 0 : n * P])
 
         def staged(t):
             run, c = divmod(t, RUN)
@@ -459,6 +447,11 @@ def tile_block_pa_t_kernel(
                 v_new = stage.tile([P, NH, RUN, DH], F32, name="v_stage")
                 stage_of[run] = (qk_new, v_new)
             return stage_of[run], c
+
+        def finished_part(t):
+            run, c = divmod(t, RUN)
+            cuts = (0, 3, 5, RUN) if run == 2 * BANDS - 1 else (0, RUN)
+            return (cuts[cuts.index(c + 1) - 1], c + 1) if c + 1 in cuts else None
 
         def finish_values(r):
             first, n = units[r]
@@ -476,8 +469,9 @@ def tile_block_pa_t_kernel(
                     op=ALU.add,
                 )
                 i += count
-                if c + count == RUN:
-                    store((first + i - 1) // RUN, 2)
+                part = finished_part(first + i - 1)
+                if part is not None:
+                    store((first + i - 1) // RUN, 2, part[0], part[1])
 
         def turn_back(r, i):
             if i >= units[r][1]:
@@ -488,7 +482,7 @@ def tile_block_pa_t_kernel(
                 for m in range(2):
                     target = out_ps[:, m, :, f * HALF : (f + 1) * HALF]
                     band, c = divmod(units[r][0] + i, WS)
-                    if f == 1 and m in BY_MATMUL and band < BANDS:
+                    if f == 1 and band < BANDS:
                         nc.tensor.matmul(
                             target, lhsT=turned_of[r][f][0][:, m, tokens],
                             rhs=turns[:, c, :].rearrange("p (h d) -> p h d", h=NH),
@@ -509,25 +503,28 @@ def tile_block_pa_t_kernel(
             t = units[r][0] + i
             tiles, c = staged(t)
             nc.scalar.copy(out=tiles[0][:, :, :, c, :], in_=turning[r, i][:])
-            if c == RUN - 1:
-                store(t // RUN, 0)
-                store(t // RUN, 1)
+            part = finished_part(t)
+            if part is not None:
+                for m in range(2):
+                    store(t // RUN, m, part[0], part[1])
 
-        def store(run, n_out):
+        def store(run, n_out, c0, c1):
             qk_stage, v_stage = stage_of[run]
             band, part = divmod(run, 2)
             o = (out_0, out_1, out_2)[n_out]
             if band < BANDS:
                 rows = o.rearrange("w h (r c) d -> h w r c d", c=WS)[
-                    :, :, band * ROWS : (band + 1) * ROWS, part * RUN : (part + 1) * RUN, :
+                    :, :, band * ROWS : (band + 1) * ROWS, part * RUN + c0 : part * RUN + c1, :
                 ]
             else:
-                rows = o.rearrange("w h (r c) d -> h w r c d", c=RUN)[:, :, 2 * BANDS * ROWS :]
+                rows = o.rearrange("w h (r c) d -> h w r c d", c=RUN)[
+                    :, :, 2 * BANDS * ROWS :, c0:c1, :
+                ]
             for h in range(NH):
                 src = v_stage[:, h] if n_out == 2 else qk_stage[:, n_out, h]
                 nc.sync.dma_start(
                     out=rows[h].rearrange("w r c d -> w r (c d)"),
-                    in_=src.rearrange("p c d -> p (c d)"),
+                    in_=src[:, c0:c1, :].rearrange("p c d -> p (c d)"),
                 )
 
         last = len(units)
@@ -535,8 +532,6 @@ def tile_block_pa_t_kernel(
             stats, norm, lace, proj, turn = (
                 s - lag if 0 <= s - lag < last else None for lag in range(5)
             )
-            if s == 2:
-                q_bias, v_bias, bias_col, w_codes, w_scales = late_constants()
             if proj is not None:
                 quantise(proj)
                 project(proj)
@@ -547,13 +542,14 @@ def tile_block_pa_t_kernel(
             if stats is not None:
                 statistics(stats, 0)
                 statistics(stats, 1)
+            if proj is not None:
+                rotate_rows(proj, 0)
+            if stats is not None:
                 finish_statistics(stats)
                 negate_mean(stats)
             if proj is not None:
-                rotate_rows(proj, 0)
-                rotate_columns(proj, 0)
+                rotate_columns(proj)
                 rotate_rows(proj, 1)
-                rotate_columns(proj, 1)
                 finish_values(proj)
                 if proj < WS // 2:
                     make_turn(2 * proj)
@@ -564,8 +560,15 @@ def tile_block_pa_t_kernel(
                     leave(turn, i)
             if stats is not None:
                 invert_deviation(stats)
+            if s == 0:
+                q_bias, v_bias = spread_biases(nc, keep, psum_t, ident, bias_rows, vrow, ones)
+                w_grouped = group_weights(nc, setup, raw)
             if norm is not None:
                 transpose_slots(norm)
+            if s == 1:
+                w_codes, w_scales = quantise_weights(nc, keep, w_grouped)
+                permutations()
+                by_row, last_col = rotary_tables(nc, keep, by_col, sign)
             if lace is not None and lace < WS // 2:
                 make_sines(2 * lace)
                 make_sines(2 * lace + 1)

@@ -40,8 +40,11 @@ def units_of_tiles():
     return units[: WS // 2] + last_group + units[WS // 2 : -1] + end
 
 
-def group_weights(nc, setup, raws):
-    grouped = setup.tile([P, 3 * E, PACK], BF16, align_bytes=64)
+def copy_on_gpsimd(nc, out, in_):
+    nc.gpsimd.tensor_scalar(out=out, in0=in_, scalar1=1.0, scalar2=0.0, op0=ALU.mult, op1=ALU.add)
+
+
+def group_weights(nc, grouped, raws):
     for n in range(2):
         src = raws[n][:].rearrange("p j (h f d) -> p f h d j", h=NH, f=2)
         for f in range(2):
@@ -50,8 +53,6 @@ def group_weights(nc, setup, raws):
                 out=grouped[:, first : first + P, :].rearrange("p (h d) j -> p h d j", h=NH),
                 in_=src[:, f],
             )
-    nc.vector.tensor_copy(out=grouped[:, 2 * E :, :], in_=raws[2][:].rearrange("p j e -> p e j"))
-    return grouped
 
 
 def quantise_weights(nc, keep, grouped):
@@ -180,7 +181,7 @@ def tile_block_pa_t_kernel(
         stage = ctx.enter_context(tc.tile_pool(name="stage", bufs=3))
         psum_t = ctx.enter_context(tc.psum_pool(name="psum_t", bufs=2))
         psum_a = ctx.enter_context(tc.psum_pool(name="psum_a", bufs=1))
-        psum_r = ctx.enter_context(tc.psum_pool(name="psum_r", bufs=2))
+        psum_r = ctx.enter_context(tc.psum_pool(name="psum_r", bufs=3))
 
         setup = ctx.enter_context(tc.tile_pool(name="setup", bufs=1))
 
@@ -206,7 +207,7 @@ def tile_block_pa_t_kernel(
         nc.vector.memset(zero[:], 0.0)
         rows_bf, vrow, ones = load_biases(nc, setup, q_b, v_b)
         raw = [keep.tile([P, PACK, E], BF16, name="raw%d" % n) for n in range(3)]
-        for tile, w in zip(raw, (q_w, k_w, v_w)):
+        for tile, w in ((raw[2], v_w), (raw[0], q_w), (raw[1], k_w)):
             nc.sync.dma_start(out=tile[:], in_=w.rearrange("(p j) e -> p j e", j=PACK))
         load(0, 4, 8)
         load(0, 8, WS)
@@ -242,16 +243,13 @@ def tile_block_pa_t_kernel(
         swap = keep.tile([P, P], F32)
         perm_last = keep.tile([P, P], F32)
 
-        def permutations():
-            for e in range(2):
-                nc.vector.tensor_copy(
-                    out=swap[:].rearrange("p (m e) -> p m e", e=2)[:, :, e],
-                    in_=ident[:].rearrange("p (m e) -> p m e", e=2)[:, :, 1 - e],
-                )
-            nc.vector.tensor_copy(
-                out=perm_last[:].rearrange("p (bi j rl hf) -> p bi j rl hf", bi=8, j=4, rl=2),
-                in_=ident[:].rearrange("p (rl j hf bi) -> p bi j rl hf", rl=2, j=4, hf=2),
+        for e in range(2):
+            copy_on_gpsimd(
+                nc, swap[:].rearrange("p (m e) -> p m e", e=2)[:, :, e],
+                ident[:].rearrange("p (m e) -> p m e", e=2)[:, :, 1 - e],
             )
+        w_grouped = setup.tile([P, 3 * E, PACK], BF16, align_bytes=64)
+        copy_on_gpsimd(nc, w_grouped[:, 2 * E :, :], raw[2][:].rearrange("p j e -> p e j"))
 
         turns = keep.tile([P, WS, P], F32)
 
@@ -396,31 +394,32 @@ def tile_block_pa_t_kernel(
                     start=True, stop=True,
                 )
             acc_of[r] = (acc_a, acc_b, acc_v)
-            turned_a0 = work.tile([P, 2, 2 * P], F32)
-            turned_a1 = work.tile([P, 2, 2 * P], F32)
-            turned_b0 = work.tile([P, 2, 2 * P], F32)
-            turned_b1 = work.tile([P, 2, 2 * P], F32)
-            turned_of[r] = ((turned_a0, turned_a1), (turned_b0, turned_b1))
+            turned_a = work.tile([P, 2, 2, 2 * P], F32)
+            turned_b = work.tile([P, 2, 2, 2 * P], F32)
+            turned_of[r] = (turned_a, turned_b)
 
         def times_table(r, f, m, tokens, table):
+            words = (tokens.stop - tokens.start) // ROWS
+            source = acc_of[r][f][:, m, tokens].rearrange("p (w r) -> p w r", r=ROWS)
+            target = turned_of[r][f][:, :, m, tokens].rearrange("p k (w r) -> p k w r", r=ROWS)
+            if m == 1:
+                shape = [P, 2, words, ROWS]
+                nc.vector.tensor_tensor(
+                    out=target, in0=source.unsqueeze(1).to_broadcast(shape),
+                    in1=table.unsqueeze(2).to_broadcast(shape), op=ALU.mult,
+                )
+                return
             for k in range(2):
-                shape = [P, (tokens.stop - tokens.start) // ROWS, ROWS]
-                spread = table[k].unsqueeze(1).to_broadcast(shape)
-                source = acc_of[r][f][:, m, tokens].rearrange("p (w r) -> p w r", r=ROWS)
-                target = turned_of[r][f][k][:, m, tokens].rearrange("p (w r) -> p w r", r=ROWS)
-                if m == 0:
-                    nc.vector.scalar_tensor_tensor(
-                        out=target, in0=source, scalar=q_bias[:, f : f + 1], in1=spread,
-                        op0=ALU.add, op1=ALU.mult,
-                    )
-                else:
-                    nc.vector.tensor_tensor(out=target, in0=source, in1=spread, op=ALU.mult)
+                nc.vector.scalar_tensor_tensor(
+                    out=target[:, k], in0=source, scalar=q_bias[:, f : f + 1],
+                    in1=table[:, k, :].unsqueeze(1).to_broadcast([P, words, ROWS]),
+                    op0=ALU.add, op1=ALU.mult,
+                )
 
         def rotate_rows(r, m):
             first, n = units[r]
             band = first // WS
-            table = [by_row[:, k, band * ROWS : (band + 1) * ROWS] for k in range(2)]
-            times_table(r, 0, m, slice(0, n * P), table)
+            times_table(r, 0, m, slice(0, n * P), by_row[:, :, band * ROWS : (band + 1) * ROWS])
 
         def rotate_columns(r):
             first, n = units[r]
@@ -429,16 +428,14 @@ def tile_block_pa_t_kernel(
                 for i in range(n):
                     c = first - BANDS * WS + i
                     for m in range(2):
-                        times_table(
-                            r, 1, m, slice(i * P, (i + 1) * P), [last_col[:, k, c, :] for k in range(2)]
-                        )
+                        times_table(r, 1, m, slice(i * P, (i + 1) * P), last_col[:, :, c, :])
                 return
-            target = turned_of[r][1][0]
+            target = turned_of[r][1]
             nc.scalar.activation(
-                out=target[:, 0, 0 : n * P], in_=acc[:, 0, 0 : n * P], func=ACT.Identity,
+                out=target[:, 0, 0, 0 : n * P], in_=acc[:, 0, 0 : n * P], func=ACT.Identity,
                 bias=q_bias[:, 1:2], scale=1.0,
             )
-            nc.scalar.copy(out=target[:, 1, 0 : n * P], in_=acc[:, 1, 0 : n * P])
+            nc.scalar.copy(out=target[:, 0, 1, 0 : n * P], in_=acc[:, 1, 0 : n * P])
 
         def staged(t):
             run, c = divmod(t, RUN)
@@ -484,14 +481,14 @@ def tile_block_pa_t_kernel(
                     band, c = divmod(units[r][0] + i, WS)
                     if f == 1 and band < BANDS:
                         nc.tensor.matmul(
-                            target, lhsT=turned_of[r][f][0][:, m, tokens],
+                            target, lhsT=turned_of[r][f][:, 0, m, tokens],
                             rhs=turns[:, c, :].rearrange("p (h d) -> p h d", h=NH),
                             start=True, stop=True,
                         )
                         continue
                     for k, order in enumerate((ident, swap)):
                         nc.tensor.matmul(
-                            target, lhsT=turned_of[r][f][k][:, m, tokens],
+                            target, lhsT=turned_of[r][f][:, k, m, tokens],
                             rhs=order[:].rearrange("p (h d) -> p h d", h=NH),
                             start=k == 0, stop=k == 1, is_transpose=True,
                         )
@@ -555,19 +552,24 @@ def tile_block_pa_t_kernel(
                     make_turn(2 * proj)
                     make_turn(2 * proj + 1)
             if turn is not None:
-                for i in range(2):
-                    turn_back(turn, i)
-                    leave(turn, i)
+                turn_back(turn, 0)
+                leave(turn, 0)
             if stats is not None:
                 invert_deviation(stats)
+            if turn is not None:
+                turn_back(turn, 1)
+                leave(turn, 1)
             if s == 0:
                 q_bias, v_bias = spread_biases(nc, keep, psum_t, ident, bias_rows, vrow, ones)
-                w_grouped = group_weights(nc, setup, raw)
+                group_weights(nc, w_grouped, raw)
             if norm is not None:
                 transpose_slots(norm)
             if s == 1:
                 w_codes, w_scales = quantise_weights(nc, keep, w_grouped)
-                permutations()
+                nc.vector.tensor_copy(
+                    out=perm_last[:].rearrange("p (bi j rl hf) -> p bi j rl hf", bi=8, j=4, rl=2),
+                    in_=ident[:].rearrange("p (rl j hf bi) -> p bi j rl hf", rl=2, j=4, hf=2),
+                )
                 by_row, last_col = rotary_tables(nc, keep, by_col, sign)
             if lace is not None and lace < WS // 2:
                 make_sines(2 * lace)

@@ -21,6 +21,8 @@ NH, DH = 4, 64
 HALF = DH // 2
 FREQS = HALF // 2
 WS = 14
+IMAGE = 56
+IMAGE_BANDS = 8
 PT = 16.0
 THETA = 10000.0
 EPS = 1e-6
@@ -29,8 +31,9 @@ BANDS = 3
 RUN = 7
 TILES = BANDS * WS + RUN
 BANK = 512
+QK_CUT, V_CUT = 4, 5
 
-FLOPS = 2 * 6272 * C * 3 * E
+FLOPS = 2 * IMAGE_BANDS * WS * IMAGE * C * 3 * E
 
 
 def units_of_tiles():
@@ -147,10 +150,10 @@ def rotary_angles(nc, setup, part_i, pos_i):
         wraps.append(wrap)
     for wrap in wraps:
         nc.vector.tensor_tensor(out=arg[:], in0=arg[:], in1=wrap[:], op=ALU.add)
-    return arg, sign
+    return arg, bits[:, 0:1], sign
 
 
-def rotary_tables(nc, keep, by_col, sign):
+def rotary_tables(nc, keep, setup, by_col, parity, sign):
     nc.vector.tensor_scalar(
         out=by_col[:, 1, :], in0=by_col[:, 1, :], scalar1=sign[:, 0:1], scalar2=None, op0=ALU.mult
     )
@@ -167,7 +170,21 @@ def rotary_tables(nc, keep, by_col, sign):
                 out=last_col[:, k, :, 2 * r : 2 * r + 2],
                 in_=by_col[:, k, :].rearrange("p (hf i) -> p i hf", hf=2),
             )
-    return by_row, last_col
+    even = setup.tile([P, 1], F32)
+    nc.vector.tensor_scalar(
+        out=even[:], in0=parity, scalar1=-1.0, scalar2=1.0, op0=ALU.mult, op1=ALU.add
+    )
+    pair_col = keep.tile([P, WS, 2], F32)
+    for e, (own, other) in enumerate(((even[:, 0:1], parity), (parity, even[:, 0:1]))):
+        part = setup.tile([P, WS], F32, name="sine_part%d" % e)
+        nc.vector.tensor_scalar(
+            out=part[:], in0=by_col[:, 1, :], scalar1=other, scalar2=None, op0=ALU.mult
+        )
+        nc.vector.scalar_tensor_tensor(
+            out=pair_col[:, :, e], in0=by_col[:, 0, :], scalar=own, in1=part[:],
+            op0=ALU.mult, op1=ALU.add,
+        )
+    return by_row, last_col, pair_col
 
 
 def tile_block_pa_t_kernel(
@@ -181,16 +198,16 @@ def tile_block_pa_t_kernel(
         stage = ctx.enter_context(tc.tile_pool(name="stage", bufs=3))
         psum_t = ctx.enter_context(tc.psum_pool(name="psum_t", bufs=2))
         psum_a = ctx.enter_context(tc.psum_pool(name="psum_a", bufs=1))
-        psum_r = ctx.enter_context(tc.psum_pool(name="psum_r", bufs=3))
-
+        psum_r = ctx.enter_context(tc.psum_pool(name="psum_r", bufs=2))
         setup = ctx.enter_context(tc.tile_pool(name="setup", bufs=1))
 
-        x_band = x.flatten_outer_dims().rearrange("(bi t) ch -> bi t ch", bi=8)
+        x_band = x.flatten_outer_dims().rearrange("(bi t) ch -> bi t ch", bi=IMAGE_BANDS)
         x_sb = keep.tile([P, TILES, C], BF16)
 
         def load(band, first, last):
             step = WS if band < BANDS else RUN
-            pixels = x_band[:, band * ROWS * 56 : band * ROWS * 56 + 16 * step, :]
+            start = band * ROWS * IMAGE
+            pixels = x_band[:, start : start + 16 * step, :]
             tile0 = band * WS
             nc.sync.dma_start(
                 out=x_sb[:, tile0 + first : tile0 + last, :].rearrange("p c ch -> p (c ch)"),
@@ -226,7 +243,7 @@ def tile_block_pa_t_kernel(
         ident = keep.tile([P, P], F32)
         make_identity(nc, ident[:])
         nc.gpsimd.memset(ones[:], 1.0)
-        arg, sign = rotary_angles(nc, setup, part_i, pos_i)
+        arg, parity, sign = rotary_angles(nc, setup, part_i, pos_i)
         by_col = keep.tile([P, 2, WS], F32)
         nc.scalar.activation(out=by_col[:], in_=arg[:], func=ACT.Sin)
         nc.scalar.activation(out=dummy[:], in_=eps[:], func=ACT.Abs_reciprocal_sqrt)
@@ -242,7 +259,6 @@ def tile_block_pa_t_kernel(
         nc.vector.tensor_copy(out=bias_rows[:], in_=rows_bf[:])
         swap = keep.tile([P, P], F32)
         perm_last = keep.tile([P, P], F32)
-
         for e in range(2):
             copy_on_gpsimd(
                 nc, swap[:].rearrange("p (m e) -> p m e", e=2)[:, :, e],
@@ -253,19 +269,22 @@ def tile_block_pa_t_kernel(
 
         turns = keep.tile([P, WS, P], F32)
 
-        sines_of = {}
+        def spread_pairs():
+            pair_ps = psum_r.tile([P, BANK], F32, tag="turn")
+            for k, order in enumerate((ident, swap)):
+                nc.tensor.matmul(
+                    pair_ps[:, 0:P], lhsT=ident[:], rhs=order[:], start=k == 0, stop=k == 1,
+                    is_transpose=True,
+                )
+            return pair_ps
 
-        def make_sines(c):
-            sines = small.tile([P, P], F32)
-            nc.scalar.activation(
-                out=sines[:], in_=swap[:], func=ACT.Copy, scale=by_col[:, 1, c : c + 1]
-            )
-            sines_of[c] = sines
-
-        def make_turn(c):
-            nc.vector.scalar_tensor_tensor(
-                out=turns[:, c, :], in0=ident[:], scalar=by_col[:, 0, c : c + 1],
-                in1=sines_of[c][:], op0=ALU.mult, op1=ALU.add,
+        def make_turns(pair_ps, c0, c1):
+            shape = [P, c1 - c0, P // 2, 2]
+            nc.vector.tensor_tensor(
+                out=turns[:, c0:c1, :].rearrange("p c (m e) -> p c m e", e=2),
+                in0=pair_ps[:, 0:P].rearrange("p (m e) -> p m e", e=2).unsqueeze(1).to_broadcast(shape),
+                in1=pair_col[:, c0:c1, :].unsqueeze(2).to_broadcast(shape),
+                op=ALU.mult,
             )
 
         units = units_of_tiles()
@@ -352,10 +371,9 @@ def tile_block_pa_t_kernel(
                         in_=planes_of[r][:, :, tokens].rearrange("p j (c i) -> p c j i", i=4),
                     )
                 else:
-                    nc.gpsimd.tensor_scalar(
-                        out=grouped[:, tokens, :],
-                        in0=planes_of[r][:, :, tokens].rearrange("p j c -> p c j"),
-                        scalar1=1.0, scalar2=0.0, op0=ALU.mult, op1=ALU.add,
+                    copy_on_gpsimd(
+                        nc, grouped[:, tokens, :],
+                        planes_of[r][:, :, tokens].rearrange("p j c -> p c j"),
                     )
             grouped_of[r] = grouped
 
@@ -374,7 +392,7 @@ def tile_block_pa_t_kernel(
             codes, scales = codes_of[r]
             acc_a = psum_a.tile([P, 2, 2 * P], F32)
             acc_b = psum_a.tile([P, 2, 2 * P], F32)
-            acc_v = psum_a.tile([P, 2, E], F32)
+            acc_v = psum_a.tile([P, 2, E], F32, bufs=2)
             for f, acc in enumerate((acc_a, acc_b)):
                 for m in range(2):
                     weights = slice((2 * m + f) * P, (2 * m + f + 1) * P)
@@ -445,9 +463,9 @@ def tile_block_pa_t_kernel(
                 stage_of[run] = (qk_new, v_new)
             return stage_of[run], c
 
-        def finished_part(t):
+        def finished_part(t, cut):
             run, c = divmod(t, RUN)
-            cuts = (0, 3, 5, RUN) if run == 2 * BANDS - 1 else (0, RUN)
+            cuts = (0, cut, RUN) if run == 2 * BANDS - 1 else (0, RUN)
             return (cuts[cuts.index(c + 1) - 1], c + 1) if c + 1 in cuts else None
 
         def finish_values(r):
@@ -466,9 +484,10 @@ def tile_block_pa_t_kernel(
                     op=ALU.add,
                 )
                 i += count
-                part = finished_part(first + i - 1)
+                done = first + i - 1
+                part = finished_part(done, V_CUT)
                 if part is not None:
-                    store((first + i - 1) // RUN, 2, part[0], part[1])
+                    store(done // RUN, 2, part[0], part[1])
 
         def turn_back(r, i):
             if i >= units[r][1]:
@@ -500,7 +519,7 @@ def tile_block_pa_t_kernel(
             t = units[r][0] + i
             tiles, c = staged(t)
             nc.scalar.copy(out=tiles[0][:, :, :, c, :], in_=turning[r, i][:])
-            part = finished_part(t)
+            part = finished_part(t, QK_CUT)
             if part is not None:
                 for m in range(2):
                     store(t // RUN, m, part[0], part[1])
@@ -539,38 +558,39 @@ def tile_block_pa_t_kernel(
             if stats is not None:
                 statistics(stats, 0)
                 statistics(stats, 1)
-            if proj is not None:
-                rotate_rows(proj, 0)
+            if turn is not None and s <= last:
+                finish_values(turn)
             if stats is not None:
                 finish_statistics(stats)
                 negate_mean(stats)
             if proj is not None:
+                rotate_rows(proj, 0)
                 rotate_columns(proj)
                 rotate_rows(proj, 1)
-                finish_values(proj)
-                if proj < WS // 2:
-                    make_turn(2 * proj)
-                    make_turn(2 * proj + 1)
+                if s >= last:
+                    finish_values(proj)
+            if s == 2:
+                make_turns(pair_ps, 0, RUN)
+            if s == 3:
+                make_turns(pair_ps, RUN, WS)
             if turn is not None:
                 turn_back(turn, 0)
                 leave(turn, 0)
             if stats is not None:
                 invert_deviation(stats)
-            if turn is not None:
-                turn_back(turn, 1)
-                leave(turn, 1)
             if s == 0:
                 q_bias, v_bias = spread_biases(nc, keep, psum_t, ident, bias_rows, vrow, ones)
+                pair_ps = spread_pairs()
                 group_weights(nc, w_grouped, raw)
             if norm is not None:
                 transpose_slots(norm)
+            if turn is not None:
+                turn_back(turn, 1)
+                leave(turn, 1)
             if s == 1:
-                w_codes, w_scales = quantise_weights(nc, keep, w_grouped)
                 nc.vector.tensor_copy(
                     out=perm_last[:].rearrange("p (bi j rl hf) -> p bi j rl hf", bi=8, j=4, rl=2),
                     in_=ident[:].rearrange("p (rl j hf bi) -> p bi j rl hf", rl=2, j=4, hf=2),
                 )
-                by_row, last_col = rotary_tables(nc, keep, by_col, sign)
-            if lace is not None and lace < WS // 2:
-                make_sines(2 * lace)
-                make_sines(2 * lace + 1)
+                by_row, last_col, pair_col = rotary_tables(nc, keep, setup, by_col, parity, sign)
+                w_codes, w_scales = quantise_weights(nc, keep, w_grouped)

@@ -269,20 +269,14 @@ def tile_block_pa_t_kernel(
 
         turns = keep.tile([P, WS, P], F32)
 
-        def spread_pairs():
-            pair_ps = psum_r.tile([P, BANK], F32, tag="turn")
-            for k, order in enumerate((ident, swap)):
-                nc.tensor.matmul(
-                    pair_ps[:, 0:P], lhsT=ident[:], rhs=order[:], start=k == 0, stop=k == 1,
-                    is_transpose=True,
-                )
-            return pair_ps
+        pair = keep.tile([P, P], F32)
+        nc.gpsimd.tensor_tensor(out=pair[:], in0=ident[:], in1=swap[:], op=ALU.add)
 
-        def make_turns(pair_ps, c0, c1):
+        def make_turns(c0, c1):
             shape = [P, c1 - c0, P // 2, 2]
-            nc.vector.tensor_tensor(
+            nc.gpsimd.tensor_tensor(
                 out=turns[:, c0:c1, :].rearrange("p c (m e) -> p c m e", e=2),
-                in0=pair_ps[:, 0:P].rearrange("p (m e) -> p m e", e=2).unsqueeze(1).to_broadcast(shape),
+                in0=pair[:].rearrange("p (m e) -> p m e", e=2).unsqueeze(1).to_broadcast(shape),
                 in1=pair_col[:, c0:c1, :].unsqueeze(2).to_broadcast(shape),
                 op=ALU.mult,
             )
@@ -320,15 +314,14 @@ def tile_block_pa_t_kernel(
             n = units[r][1]
             mean_var = stats_of[r][1]
             minus_mean = small.tile([P, 2], F32)
-            nc.gpsimd.tensor_scalar(
-                out=minus_mean[:, 0:n], in0=mean_var[:, 0:n, 0], scalar1=-1.0, scalar2=0.0,
-                op0=ALU.mult, op1=ALU.add,
+            nc.scalar.activation(
+                out=minus_mean[:, 0:n], in_=mean_var[:, 0:n, 0], func=ACT.Copy, scale=-1.0
             )
             stats_of[r].append(minus_mean)
 
         def normalise(r):
             first, n = units[r]
-            minus_mean, rstd = stats_of[r][2:4]
+            rstd, minus_mean = stats_of[r][2:4]
             normed = work.tile([P, 2, C], F32)
             for i in range(n):
                 nc.gpsimd.tensor_scalar(
@@ -562,25 +555,22 @@ def tile_block_pa_t_kernel(
                 finish_values(turn)
             if stats is not None:
                 finish_statistics(stats)
-                negate_mean(stats)
             if proj is not None:
                 rotate_rows(proj, 0)
                 rotate_columns(proj)
                 rotate_rows(proj, 1)
                 if s >= last:
                     finish_values(proj)
-            if s == 2:
-                make_turns(pair_ps, 0, RUN)
-            if s == 3:
-                make_turns(pair_ps, RUN, WS)
+            if 2 <= s < 2 + WS // 2:
+                make_turns(units[s - 2][0], units[s - 2][0] + 2)
             if turn is not None:
                 turn_back(turn, 0)
                 leave(turn, 0)
             if stats is not None:
                 invert_deviation(stats)
+                negate_mean(stats)
             if s == 0:
                 q_bias, v_bias = spread_biases(nc, keep, psum_t, ident, bias_rows, vrow, ones)
-                pair_ps = spread_pairs()
                 group_weights(nc, w_grouped, raw)
             if norm is not None:
                 transpose_slots(norm)

@@ -40,7 +40,9 @@ def units_of_tiles():
     units = [(2 * u, 2) for u in range(BANDS * WS // 2)]
     last_group = [(BANDS * WS + i, min(2, RUN - i)) for i in range(0, RUN, 2)]
     end = [(BANDS * WS - 2, 1), (BANDS * WS - 1, 1)]
-    return units[: WS // 2] + last_group + units[WS // 2 : -1] + end
+    start = WS // 2
+    turns = [unit for pair in zip(last_group, units[start:]) for unit in pair]
+    return units[:start] + turns + units[start + len(last_group) : -1] + end
 
 
 def copy_on_gpsimd(nc, out, in_):

@@ -61,8 +61,8 @@ def group_weights(nc, grouped, raws):
 
 
 def quantise_weights(nc, keep, grouped):
-    w_codes = keep.tile([P, 3 * E], U32, align_bytes=64)
-    w_scales = keep.tile([P, 3 * E], U8, align_bytes=64)
+    w_codes = keep.tile([P, 3 * E], U32, align_bytes=256)
+    w_scales = keep.tile([P, 3 * E], U8, align_bytes=256)
     for first, last in ((0, 2 * E), (2 * E, 3 * E)):
         nc.vector.quantize_mx(
             out=w_codes[:, first:last].bitcast(FP8X4),
@@ -100,7 +100,7 @@ def spread_biases(nc, keep, psum, ident, rows, vrow, ones):
     nc.tensor.matmul(vb_ps[:, 0:E], lhsT=ones[:], rhs=vrow[:], start=True, stop=True)
     q_bias = keep.tile([P, 2], F32)
     nc.vector.tensor_copy(out=q_bias[:], in_=cols_ps[:, 0:2])
-    v_bias = keep.tile([P, E], F32)
+    v_bias = keep.tile([P, E], F32, align_bytes=256)
     nc.vector.tensor_copy(out=v_bias[:], in_=vb_ps[:, 0:E])
     return q_bias, v_bias
 
@@ -159,13 +159,13 @@ def rotary_tables(nc, keep, setup, by_col, parity, sign):
     nc.vector.tensor_scalar(
         out=by_col[:, 1, :], in0=by_col[:, 1, :], scalar1=sign[:, 0:1], scalar2=None, op0=ALU.mult
     )
-    by_row = keep.tile([P, 2, (BANDS + 1) * ROWS], F32)
+    by_row = keep.tile([P, 2, (BANDS + 1) * ROWS], F32, align_bytes=256)
     nc.vector.tensor_copy(out=by_row[:, :, 0 : BANDS * ROWS], in_=by_col[:, :, 0 : BANDS * ROWS])
     nc.vector.tensor_copy(
         out=by_row[:, :, BANDS * ROWS :].rearrange("p k (r h) -> p k r h", h=2),
         in_=by_col[:, :, BANDS * ROWS :].unsqueeze(3).to_broadcast([P, 2, 2, 2]),
     )
-    last_col = keep.tile([P, 2, RUN, ROWS], F32)
+    last_col = keep.tile([P, 2, RUN, ROWS], F32, align_bytes=256)
     for k in range(2):
         for r in range(2):
             nc.vector.tensor_copy(
@@ -176,7 +176,7 @@ def rotary_tables(nc, keep, setup, by_col, parity, sign):
     nc.vector.tensor_scalar(
         out=even[:], in0=parity, scalar1=-1.0, scalar2=1.0, op0=ALU.mult, op1=ALU.add
     )
-    pair_col = keep.tile([P, WS, 2], F32)
+    pair_col = keep.tile([P, WS, 2], F32, align_bytes=256)
     for e, (own, other) in enumerate(((even[:, 0:1], parity), (parity, even[:, 0:1]))):
         part = setup.tile([P, WS], F32, name="sine_part%d" % e)
         nc.vector.tensor_scalar(
@@ -204,7 +204,7 @@ def tile_block_pa_t_kernel(
         setup = ctx.enter_context(tc.tile_pool(name="setup", bufs=1))
 
         x_band = x.flatten_outer_dims().rearrange("(bi t) ch -> bi t ch", bi=IMAGE_BANDS)
-        x_sb = keep.tile([P, TILES, C], BF16)
+        x_sb = keep.tile([P, TILES, C], BF16, align_bytes=256)
 
         def load(band, first, last):
             step = WS if band < BANDS else RUN
@@ -225,7 +225,7 @@ def tile_block_pa_t_kernel(
         zero = setup.tile([P, 1], F32)
         nc.vector.memset(zero[:], 0.0)
         rows_bf, vrow, ones = load_biases(nc, setup, q_b, v_b)
-        raw = [keep.tile([P, PACK, E], BF16, name="raw%d" % n) for n in range(3)]
+        raw = [keep.tile([P, PACK, E], BF16, name="raw%d" % n, align_bytes=256) for n in range(3)]
         for tile, w in ((raw[2], v_w), (raw[0], q_w), (raw[1], k_w)):
             nc.sync.dma_start(out=tile[:], in_=w.rearrange("(p j) e -> p j e", j=PACK))
         load(0, 4, 8)
@@ -242,14 +242,14 @@ def tile_block_pa_t_kernel(
         nc.gpsimd.iota(part_i[:], pattern=[[0, 1]], base=0, channel_multiplier=1)
         pos_i = setup.tile([P, WS], I32)
         nc.gpsimd.iota(pos_i[:], pattern=[[1, WS]], base=0, channel_multiplier=0)
-        ident = keep.tile([P, P], F32)
+        ident = keep.tile([P, P], F32, align_bytes=256)
         make_identity(nc, ident[:])
         nc.gpsimd.memset(ones[:], 1.0)
         arg, parity, sign = rotary_angles(nc, setup, part_i, pos_i)
         by_col = keep.tile([P, 2, WS], F32)
         nc.scalar.activation(out=by_col[:], in_=arg[:], func=ACT.Sin)
         nc.scalar.activation(out=dummy[:], in_=eps[:], func=ACT.Abs_reciprocal_sqrt)
-        perm = keep.tile([P, P], F32)
+        perm = keep.tile([P, P], F32, align_bytes=256)
         nc.vector.tensor_copy(
             out=perm[:].rearrange("p (bi j r) -> p bi j r", bi=8, j=4),
             in_=ident[:].rearrange("p (r j bi) -> p bi j r", r=ROWS, j=4),
@@ -259,19 +259,19 @@ def tile_block_pa_t_kernel(
             nc.vector.tensor_copy(out=ln_cols[:, n * PACK : (n + 1) * PACK], in_=tile[:])
         bias_rows = setup.tile([P, P], F32)
         nc.vector.tensor_copy(out=bias_rows[:], in_=rows_bf[:])
-        swap = keep.tile([P, P], F32)
-        perm_last = keep.tile([P, P], F32)
+        swap = keep.tile([P, P], F32, align_bytes=256)
+        perm_last = keep.tile([P, P], F32, align_bytes=256)
         for e in range(2):
             copy_on_gpsimd(
                 nc, swap[:].rearrange("p (m e) -> p m e", e=2)[:, :, e],
                 ident[:].rearrange("p (m e) -> p m e", e=2)[:, :, 1 - e],
             )
-        w_grouped = setup.tile([P, 3 * E, PACK], BF16, align_bytes=64)
+        w_grouped = setup.tile([P, 3 * E, PACK], BF16, align_bytes=256)
         copy_on_gpsimd(nc, w_grouped[:, 2 * E :, :], raw[2][:].rearrange("p j e -> p e j"))
 
-        turns = keep.tile([P, WS, P], F32)
+        turns = keep.tile([P, WS, P], F32, align_bytes=256)
 
-        pair = keep.tile([P, P], F32)
+        pair = keep.tile([P, P], F32, align_bytes=256)
         nc.gpsimd.tensor_tensor(out=pair[:], in0=ident[:], in1=swap[:], op=ALU.add)
 
         def make_turns(c0, c1):
@@ -324,7 +324,7 @@ def tile_block_pa_t_kernel(
         def normalise(r):
             first, n = units[r]
             rstd, minus_mean = stats_of[r][2:4]
-            normed = work.tile([P, 2, C], F32)
+            normed = work.tile([P, 2, C], F32, align_bytes=256)
             for i in range(n):
                 nc.gpsimd.tensor_scalar(
                     out=normed[:, i, :].rearrange("p (j k) -> p j k", j=PACK),
@@ -337,7 +337,7 @@ def tile_block_pa_t_kernel(
         def transpose_slots(r):
             first, n = units[r]
             normed = normed_of[r]
-            planes = work.tile([P, PACK, 2 * P], BF16)
+            planes = work.tile([P, PACK, 2 * P], BF16, align_bytes=256)
             order = perm if first < BANDS * WS else perm_last
             for pair in range(2):
                 xt = psum_t.tile([P, 2, 2 * P], F32, tag="xt")
@@ -357,7 +357,7 @@ def tile_block_pa_t_kernel(
 
         def interleave(r):
             n = units[r][1]
-            grouped = work.tile([P, 2 * P, PACK], BF16, align_bytes=64)
+            grouped = work.tile([P, 2 * P, PACK], BF16, align_bytes=256)
             for i in range(n):
                 tokens = slice(i * P, (i + 1) * P)
                 if i == 1:
@@ -374,8 +374,8 @@ def tile_block_pa_t_kernel(
 
         def quantise(r):
             n = units[r][1]
-            codes = work.tile([P, 2 * P], U32, align_bytes=64)
-            scales = work.tile([P, 2 * P], U8, align_bytes=64)
+            codes = work.tile([P, 2 * P], U32, align_bytes=256)
+            scales = work.tile([P, 2 * P], U8, align_bytes=256)
             nc.vector.quantize_mx(
                 out=codes[:, 0 : n * P].bitcast(FP8X4), scales=scales[:, 0 : n * P],
                 in_=grouped_of[r][:, 0 : n * P, :].rearrange("p t j -> p (t j)"),
@@ -407,8 +407,8 @@ def tile_block_pa_t_kernel(
                     start=True, stop=True,
                 )
             acc_of[r] = (acc_a, acc_b, acc_v)
-            turned_a = work.tile([P, 2, 2, 2 * P], F32)
-            turned_b = work.tile([P, 2, 2, 2 * P], F32)
+            turned_a = work.tile([P, 2, 2, 2 * P], F32, align_bytes=256)
+            turned_b = work.tile([P, 2, 2, 2 * P], F32, align_bytes=256)
             turned_of[r] = (turned_a, turned_b)
 
         def times_table(r, f, m, tokens, table):
@@ -453,8 +453,8 @@ def tile_block_pa_t_kernel(
         def staged(t):
             run, c = divmod(t, RUN)
             if run not in stage_of:
-                qk_new = stage.tile([P, 2, NH, RUN, DH], F32, name="qk_stage")
-                v_new = stage.tile([P, NH, RUN, DH], F32, name="v_stage")
+                qk_new = stage.tile([P, 2, NH, RUN, DH], F32, name="qk_stage", align_bytes=256)
+                v_new = stage.tile([P, NH, RUN, DH], F32, name="v_stage", align_bytes=256)
                 stage_of[run] = (qk_new, v_new)
             return stage_of[run], c
 

@@ -460,7 +460,9 @@ def tile_block_pa_t_kernel(
 
         def finished_part(t, cut):
             run, c = divmod(t, RUN)
-            cuts = (0, cut, RUN) if run == 2 * BANDS - 1 else (0, RUN)
+            cuts = (0, RUN)
+            if run == 2 * BANDS - 2: cuts = (0,4,7) if cut == QK_CUT else (0,4,7)
+            if run == 2 * BANDS - 1: cuts = (0,3,7) if cut == QK_CUT else (0,7)
             return (cuts[cuts.index(c + 1) - 1], c + 1) if c + 1 in cuts else None
 
         def finish_values(r):

import math
from contextlib import ExitStack

import concourse.mybir as mybir
from concourse.masks import make_identity

F32 = mybir.dt.float32
BF16 = mybir.dt.bfloat16
I32 = mybir.dt.int32
U32 = mybir.dt.uint32
U8 = mybir.dt.uint8
FP8X4 = mybir.dt.float8_e4m3fn_x4
ALU = mybir.AluOpType
ACT = mybir.ActivationFunctionType

P = 128
C = 512
PACK = 4
E = 256
NH, DH = 4, 64
HALF = DH // 2
FREQS = HALF // 2
WS = 14
IMAGE = 56
IMAGE_BANDS = 8
PT = 16.0
THETA = 10000.0
EPS = 1e-6
ROWS = 4
BANDS = 3
RUN = 7
TILES = BANDS * WS + RUN
BANK = 512
QK_CUT, V_CUT = 4, 5

FLOPS = 2 * IMAGE_BANDS * WS * IMAGE * C * 3 * E


def units_of_tiles():
    units = [(2 * u, 2) for u in range(BANDS * WS // 2)]
    last_group = [(BANDS * WS + i, min(2, RUN - i)) for i in range(0, RUN, 2)]
    end = [(BANDS * WS - 2, 1), (BANDS * WS - 1, 1)]
    start = WS // 2
    turns = [unit for pair in zip(last_group, units[start:]) for unit in pair]
    return units[:start] + turns + units[start + len(last_group) : -1] + end


def copy_on_gpsimd(nc, out, in_):
    nc.gpsimd.tensor_scalar(out=out, in0=in_, scalar1=1.0, scalar2=0.0, op0=ALU.mult, op1=ALU.add)


def group_weights(nc, grouped, raws):
    for n in range(2):
        src = raws[n][:].rearrange("p j (h f d) -> p f h d j", h=NH, f=2)
        for f in range(2):
            first = n * E + f * P
            nc.scalar.copy(
                out=grouped[:, first : first + P, :].rearrange("p (h d) j -> p h d j", h=NH),
                in_=src[:, f],
            )


def quantise_weights(nc, keep, grouped):
    w_codes = keep.tile([P, 3 * E], U32, align_bytes=256)
    w_scales = keep.tile([P, 3 * E], U8, align_bytes=256)
    for first, last in ((0, 2 * E), (2 * E, 3 * E)):
        nc.vector.quantize_mx(
            out=w_codes[:, first:last].bitcast(FP8X4),
            scales=w_scales[:, first:last],
            in_=grouped[:, first:last, :].rearrange("p e j -> p (e j)"),
        )
    return w_codes, w_scales


def load_layer_norm(nc, setup, ln1_w, ln1_b):
    cols = [setup.tile([P, PACK], BF16, name="cols%d" % n) for n in range(2)]
    for tile, vec in zip(cols, (ln1_w, ln1_b)):
        nc.sync.dma_start(out=tile[:], in_=vec.rearrange("(p j) -> p j", j=PACK))
    return cols


def load_biases(nc, setup, q_b, v_b):
    rows_bf = setup.tile([P, P], BF16)
    nc.vector.memset(rows_bf[:], 0.0)
    nc.sync.dma_start(
        out=rows_bf[0:2, :].rearrange("f (h d) -> f h d", h=NH),
        in_=q_b.rearrange("(h f d) -> f h d", h=NH, f=2),
    )
    vrow = setup.tile([P, E], BF16)
    nc.vector.memset(vrow[:], 0.0)
    nc.sync.dma_start(out=vrow[0:1, :], in_=v_b.unsqueeze(0))
    ones = setup.tile([P, P], BF16)
    return rows_bf, vrow, ones


def spread_biases(nc, keep, psum, ident, rows, vrow, ones):
    cols_ps = psum.tile([P, BANK], F32, tag="xt")
    nc.tensor.transpose(cols_ps[:, 0:P], rows[:], ident[:])
    vb_ps = psum.tile([P, BANK], F32, tag="xt")
    nc.tensor.matmul(vb_ps[:, 0:E], lhsT=ones[:], rhs=vrow[:], start=True, stop=True)
    q_bias = keep.tile([P, 2], F32)
    nc.vector.tensor_copy(out=q_bias[:], in_=cols_ps[:, 0:2])
    v_bias = keep.tile([P, E], F32, align_bytes=256)
    nc.vector.tensor_copy(out=v_bias[:], in_=vb_ps[:, 0:E])
    return q_bias, v_bias


def rotary_angles(nc, setup, part_i, pos_i):
    pos = setup.tile([P, WS], F32)
    nc.vector.tensor_copy(out=pos[:], in_=pos_i[:])
    bits_i = setup.tile([P, 5], I32)
    for b in range(5):
        nc.vector.tensor_scalar(
            out=bits_i[:, b : b + 1], in0=part_i[:], scalar1=b, scalar2=1,
            op0=ALU.logical_shift_right, op1=ALU.bitwise_and,
        )
    bits = setup.tile([P, 5], F32)
    nc.vector.tensor_copy(out=bits[:], in_=bits_i[:])
    factors = setup.tile([P, 4], F32)
    for b in range(4):
        nc.vector.tensor_scalar(
            out=factors[:, b : b + 1], in0=bits[:, b + 1 : b + 2],
            scalar1=THETA ** (-(2**b) / FREQS) - 1.0, scalar2=1.0, op0=ALU.mult, op1=ALU.add,
        )
    pairs = setup.tile([P, 2], F32)
    nc.vector.tensor_tensor(
        out=pairs[:], in0=factors[:, 0:2], in1=factors[:, 2:4], op=ALU.mult
    )
    freq = setup.tile([P, 1], F32)
    nc.vector.scalar_tensor_tensor(
        out=freq[:], in0=pairs[:, 0:1], scalar=PT / WS, in1=pairs[:, 1:2],
        op0=ALU.mult, op1=ALU.mult,
    )
    sign = setup.tile([P, 1], F32)
    nc.vector.tensor_scalar(
        out=sign[:], in0=bits[:, 0:1], scalar1=-2.0, scalar2=1.0, op0=ALU.mult, op1=ALU.add
    )
    arg = setup.tile([P, 2, WS], F32)
    for k, offset in enumerate((math.pi / 2, 0.0)):
        nc.vector.tensor_scalar(
            out=arg[:, k, :], in0=pos[:], scalar1=freq[:, 0:1], scalar2=offset,
            op0=ALU.mult, op1=ALU.add,
        )
    largest = (WS - 1) * PT / WS + math.pi / 2
    wraps = []
    for turn in range(math.ceil((largest - math.pi) / (2 * math.pi))):
        wrap = setup.tile([P, 2, WS], F32, name="wrap%d" % turn)
        nc.vector.tensor_scalar(
            out=wrap[:], in0=arg[:], scalar1=(2 * turn + 1) * math.pi, scalar2=-2 * math.pi,
            op0=ALU.is_gt, op1=ALU.mult,
        )
        wraps.append(wrap)
    for wrap in wraps:
        nc.vector.tensor_tensor(out=arg[:], in0=arg[:], in1=wrap[:], op=ALU.add)
    return arg, bits[:, 0:1], sign


def rotary_tables(nc, keep, setup, by_col, parity, sign):
    nc.vector.tensor_scalar(
        out=by_col[:, 1, :], in0=by_col[:, 1, :], scalar1=sign[:, 0:1], scalar2=None, op0=ALU.mult
    )
    by_row = keep.tile([P, 2, (BANDS + 1) * ROWS], F32, align_bytes=256)
    nc.vector.tensor_copy(out=by_row[:, :, 0 : BANDS * ROWS], in_=by_col[:, :, 0 : BANDS * ROWS])
    nc.vector.tensor_copy(
        out=by_row[:, :, BANDS * ROWS :].rearrange("p k (r h) -> p k r h", h=2),
        in_=by_col[:, :, BANDS * ROWS :].unsqueeze(3).to_broadcast([P, 2, 2, 2]),
    )
    last_col = keep.tile([P, 2, RUN, ROWS], F32, align_bytes=256)
    for k in range(2):
        for r in range(2):
            nc.vector.tensor_copy(
                out=last_col[:, k, :, 2 * r : 2 * r + 2],
                in_=by_col[:, k, :].rearrange("p (hf i) -> p i hf", hf=2),
            )
    even = setup.tile([P, 1], F32)
    nc.vector.tensor_scalar(
        out=even[:], in0=parity, scalar1=-1.0, scalar2=1.0, op0=ALU.mult, op1=ALU.add
    )
    pair_col = keep.tile([P, WS, 2], F32, align_bytes=256)
    for e, (own, other) in enumerate(((even[:, 0:1], parity), (parity, even[:, 0:1]))):
        part = setup.tile([P, WS], F32, name="sine_part%d" % e)
        nc.vector.tensor_scalar(
            out=part[:], in0=by_col[:, 1, :], scalar1=other, scalar2=None, op0=ALU.mult
        )
        nc.vector.scalar_tensor_tensor(
            out=pair_col[:, :, e], in0=by_col[:, 0, :], scalar=own, in1=part[:],
            op0=ALU.mult, op1=ALU.add,
        )
    return by_row, last_col, pair_col


def tile_block_pa_t_kernel(
    tc, x, ln1_w, ln1_b, q_w, q_b, k_w, v_w, v_b, out_0, out_1, out_2
):
    nc = tc.nc
    with ExitStack() as ctx:
        keep = ctx.enter_context(tc.tile_pool(name="keep", bufs=1))
        work = ctx.enter_context(tc.tile_pool(name="work", bufs=2))
        small = ctx.enter_context(tc.tile_pool(name="small", bufs=4))
        stage = ctx.enter_context(tc.tile_pool(name="stage", bufs=3))
        psum_t = ctx.enter_context(tc.psum_pool(name="psum_t", bufs=2))
        psum_a = ctx.enter_context(tc.psum_pool(name="psum_a", bufs=1))
        psum_r = ctx.enter_context(tc.psum_pool(name="psum_r", bufs=2))
        setup = ctx.enter_context(tc.tile_pool(name="setup", bufs=1))

        x_band = x.flatten_outer_dims().rearrange("(bi t) ch -> bi t ch", bi=IMAGE_BANDS)
        x_sb = keep.tile([P, TILES, C], BF16, align_bytes=256)

        def load(band, first, last):
            step = WS if band < BANDS else RUN
            start = band * ROWS * IMAGE
            pixels = x_band[:, start : start + 16 * step, :]
            tile0 = band * WS
            nc.sync.dma_start(
                out=x_sb[:, tile0 + first : tile0 + last, :].rearrange("p c ch -> p (c ch)"),
                in_=pixels.rearrange("bi (q c) ch -> q bi c ch", q=16)[:, :, first:last, :].rearrange(
                    "q bi c ch -> q bi (c ch)"
                ),
            )

        ctx.enter_context(tc.manual_schedule())
        load(0, 0, 2)
        ln_bf = load_layer_norm(nc, setup, ln1_w, ln1_b)
        load(0, 2, 4)
        zero = setup.tile([P, 1], F32)
        nc.vector.memset(zero[:], 0.0)
        rows_bf, vrow, ones = load_biases(nc, setup, q_b, v_b)
        raw = [keep.tile([P, PACK, E], BF16, name="raw%d" % n, align_bytes=256) for n in range(3)]
        for tile, w in ((raw[2], v_w), (raw[0], q_w), (raw[1], k_w)):
            nc.sync.dma_start(out=tile[:], in_=w.rearrange("(p j) e -> p j e", j=PACK))
        load(0, 4, 8)
        load(0, 8, WS)
        load(3, 0, RUN)
        load(1, 0, WS)
        load(2, 0, WS)

        dummy = setup.tile([P, 1], F32)
        nc.scalar.activation(out=dummy[:], in_=zero[:], func=ACT.Sin)
        eps = keep.tile([P, 1], F32)
        nc.vector.tensor_scalar_add(out=eps[:], in0=zero[:], scalar1=EPS)
        part_i = setup.tile([P, 1], I32)
        nc.gpsimd.iota(part_i[:], pattern=[[0, 1]], base=0, channel_multiplier=1)
        pos_i = setup.tile([P, WS], I32)
        nc.gpsimd.iota(pos_i[:], pattern=[[1, WS]], base=0, channel_multiplier=0)
        ident = keep.tile([P, P], F32, align_bytes=256)
        make_identity(nc, ident[:])
        nc.gpsimd.memset(ones[:], 1.0)
        arg, parity, sign = rotary_angles(nc, setup, part_i, pos_i)
        by_col = keep.tile([P, 2, WS], F32)
        nc.scalar.activation(out=by_col[:], in_=arg[:], func=ACT.Sin)
        nc.scalar.activation(out=dummy[:], in_=eps[:], func=ACT.Abs_reciprocal_sqrt)
        perm = keep.tile([P, P], F32, align_bytes=256)
        nc.vector.tensor_copy(
            out=perm[:].rearrange("p (bi j r) -> p bi j r", bi=8, j=4),
            in_=ident[:].rearrange("p (r j bi) -> p bi j r", r=ROWS, j=4),
        )
        ln_cols = keep.tile([P, 2 * PACK], F32)
        for n, tile in enumerate(ln_bf):
            nc.vector.tensor_copy(out=ln_cols[:, n * PACK : (n + 1) * PACK], in_=tile[:])
        bias_rows = setup.tile([P, P], F32)
        nc.vector.tensor_copy(out=bias_rows[:], in_=rows_bf[:])
        swap = keep.tile([P, P], F32, align_bytes=256)
        perm_last = keep.tile([P, P], F32, align_bytes=256)
        for e in range(2):
            copy_on_gpsimd(
                nc, swap[:].rearrange("p (m e) -> p m e", e=2)[:, :, e],
                ident[:].rearrange("p (m e) -> p m e", e=2)[:, :, 1 - e],
            )
        w_grouped = setup.tile([P, 3 * E, PACK], BF16, align_bytes=256)
        copy_on_gpsimd(nc, w_grouped[:, 2 * E :, :], raw[2][:].rearrange("p j e -> p e j"))

        turns = keep.tile([P, WS, P], F32, align_bytes=256)

        pair = keep.tile([P, P], F32, align_bytes=256)
        nc.gpsimd.tensor_tensor(out=pair[:], in0=ident[:], in1=swap[:], op=ALU.add)

        def make_turns(c0, c1):
            shape = [P, c1 - c0, P // 2, 2]
            nc.gpsimd.tensor_tensor(
                out=turns[:, c0:c1, :].rearrange("p c (m e) -> p c m e", e=2),
                in0=pair[:].rearrange("p (m e) -> p m e", e=2).unsqueeze(1).to_broadcast(shape),
                in1=pair_col[:, c0:c1, :].unsqueeze(2).to_broadcast(shape),
                op=ALU.mult,
            )

        units = units_of_tiles()
        stats_of, normed_of, planes_of, grouped_of = {}, {}, {}, {}
        codes_of, acc_of, turned_of, stage_of, turning = {}, {}, {}, {}, {}

        def statistics(r, i):
            first, n = units[r]
            if i == 0:
                six = small.tile([P, 2, 6], F32)
                mean_var = small.tile([P, 2, 2], F32)
                stats_of[r] = [six, mean_var]
            if i < n:
                nc.vector.bn_stats(out=stats_of[r][0][:, i, :], in_=x_sb[:, first + i, :])

        def finish_statistics(r):
            n = units[r][1]
            six, mean_var = stats_of[r]
            for i in range(n):
                nc.vector.bn_aggr(out=mean_var[:, i, :], in_=six[:, i, :])

        def invert_deviation(r):
            n = units[r][1]
            mean_var = stats_of[r][1]
            rstd = small.tile([P, 2], F32)
            nc.scalar.activation(
                out=rstd[:, 0:n], in_=mean_var[:, 0:n, 1], func=ACT.Abs_reciprocal_sqrt,
                bias=eps[:, 0:1], scale=1.0,
            )
            stats_of[r].append(rstd)

        def negate_mean(r):
            n = units[r][1]
            mean_var = stats_of[r][1]
            minus_mean = small.tile([P, 2], F32)
            nc.scalar.activation(
                out=minus_mean[:, 0:n], in_=mean_var[:, 0:n, 0], func=ACT.Copy, scale=-1.0
            )
            stats_of[r].append(minus_mean)

        def normalise(r):
            first, n = units[r]
            rstd, minus_mean = stats_of[r][2:4]
            normed = work.tile([P, 2, C], F32, align_bytes=256)
            for i in range(n):
                nc.gpsimd.tensor_scalar(
                    out=normed[:, i, :].rearrange("p (j k) -> p j k", j=PACK),
                    in0=x_sb[:, first + i, :].rearrange("p (k j) -> p j k", j=PACK),
                    scalar1=minus_mean[:, i : i + 1], scalar2=rstd[:, i : i + 1],
                    op0=ALU.add, op1=ALU.mult,
                )
            normed_of[r] = normed

        def transpose_slots(r):
            first, n = units[r]
            normed = normed_of[r]
            planes = work.tile([P, PACK, 2 * P], BF16, align_bytes=256)
            order = perm if first < BANDS * WS else perm_last
            for pair in range(2):
                xt = psum_t.tile([P, 2, 2 * P], F32, tag="xt")
                for jj in range(2):
                    j = 2 * pair + jj
                    for i in range(n):
                        nc.tensor.transpose(
                            xt[:, jj, i * P : (i + 1) * P], normed[:, i, j * P : (j + 1) * P], order[:]
                        )
                for jj in range(2):
                    j = 2 * pair + jj
                    nc.scalar.activation(
                        out=planes[:, j, 0 : n * P], in_=xt[:, jj, 0 : n * P], func=ACT.Identity,
                        bias=ln_cols[:, PACK + j : PACK + j + 1], scale=ln_cols[:, j : j + 1],
                    )
            planes_of[r] = planes

        def interleave(r):
            n = units[r][1]
            grouped = work.tile([P, 2 * P, PACK], BF16, align_bytes=256)
            for i in range(n):
                tokens = slice(i * P, (i + 1) * P)
                if i == 1:
                    nc.scalar.copy(
                        out=grouped[:, tokens, :].rearrange("p (c i) j -> p c j i", i=4),
                        in_=planes_of[r][:, :, tokens].rearrange("p j (c i) -> p c j i", i=4),
                    )
                else:
                    copy_on_gpsimd(
                        nc, grouped[:, tokens, :],
                        planes_of[r][:, :, tokens].rearrange("p j c -> p c j"),
                    )
            grouped_of[r] = grouped

        def quantise(r):
            n = units[r][1]
            codes = work.tile([P, 2 * P], U32, align_bytes=256)
            scales = work.tile([P, 2 * P], U8, align_bytes=256)
            nc.vector.quantize_mx(
                out=codes[:, 0 : n * P].bitcast(FP8X4), scales=scales[:, 0 : n * P],
                in_=grouped_of[r][:, 0 : n * P, :].rearrange("p t j -> p (t j)"),
            )
            codes_of[r] = (codes, scales)

        def project(r):
            n = units[r][1]
            codes, scales = codes_of[r]
            acc_a = psum_a.tile([P, 2, 2 * P], F32)
            acc_b = psum_a.tile([P, 2, 2 * P], F32)
            acc_v = psum_a.tile([P, 2, E], F32, bufs=2)
            for f, acc in enumerate((acc_a, acc_b)):
                for m in range(2):
                    weights = slice((2 * m + f) * P, (2 * m + f + 1) * P)
                    nc.tensor.matmul_mx(
                        out=acc[:, m, 0 : n * P],
                        lhsT=w_codes[:, weights].bitcast(FP8X4), lhsT_scale=w_scales[:, weights],
                        rhs=codes[:, 0 : n * P].bitcast(FP8X4), rhs_scale=scales[:, 0 : n * P],
                        start=True, stop=True,
                    )
            weights = slice(2 * E, 3 * E)
            for i in range(n):
                tokens = slice(i * P, (i + 1) * P)
                nc.tensor.matmul_mx(
                    out=acc_v[:, i, :],
                    lhsT=codes[:, tokens].bitcast(FP8X4), lhsT_scale=scales[:, tokens],
                    rhs=w_codes[:, weights].bitcast(FP8X4), rhs_scale=w_scales[:, weights],
                    start=True, stop=True,
                )
            acc_of[r] = (acc_a, acc_b, acc_v)
            turned_a = work.tile([P, 2, 2, 2 * P], F32, align_bytes=256)
            turned_b = work.tile([P, 2, 2, 2 * P], F32, align_bytes=256)
            turned_of[r] = (turned_a, turned_b)

        def times_table(r, f, m, tokens, table):
            words = (tokens.stop - tokens.start) // ROWS
            source = acc_of[r][f][:, m, tokens].rearrange("p (w r) -> p w r", r=ROWS)
            target = turned_of[r][f][:, :, m, tokens].rearrange("p k (w r) -> p k w r", r=ROWS)
            if m == 1:
                shape = [P, 2, words, ROWS]
                nc.vector.tensor_tensor(
                    out=target, in0=source.unsqueeze(1).to_broadcast(shape),
                    in1=table.unsqueeze(2).to_broadcast(shape), op=ALU.mult,
                )
                return
            for k in range(2):
                nc.vector.scalar_tensor_tensor(
                    out=target[:, k], in0=source, scalar=q_bias[:, f : f + 1],
                    in1=table[:, k, :].unsqueeze(1).to_broadcast([P, words, ROWS]),
                    op0=ALU.add, op1=ALU.mult,
                )

        def rotate_rows(r, m):
            first, n = units[r]
            band = first // WS
            times_table(r, 0, m, slice(0, n * P), by_row[:, :, band * ROWS : (band + 1) * ROWS])

        def rotate_columns(r):
            first, n = units[r]
            acc = acc_of[r][1]
            if first >= BANDS * WS:
                for i in range(n):
                    c = first - BANDS * WS + i
                    for m in range(2):
                        times_table(r, 1, m, slice(i * P, (i + 1) * P), last_col[:, :, c, :])
                return
            target = turned_of[r][1]
            nc.scalar.activation(
                out=target[:, 0, 0, 0 : n * P], in_=acc[:, 0, 0 : n * P], func=ACT.Identity,
                bias=q_bias[:, 1:2], scale=1.0,
            )
            nc.scalar.copy(out=target[:, 0, 1, 0 : n * P], in_=acc[:, 1, 0 : n * P])

        def staged(t):
            run, c = divmod(t, RUN)
            if run not in stage_of:
                qk_new = stage.tile([P, 2, NH, RUN, DH], F32, name="qk_stage", align_bytes=256)
                v_new = stage.tile([P, NH, RUN, DH], F32, name="v_stage", align_bytes=256)
                stage_of[run] = (qk_new, v_new)
            return stage_of[run], c

        def finished_part(t, cut):
            run, c = divmod(t, RUN)
            cuts = (0, RUN)
            if run == 2 * BANDS - 2: cuts = (0,4,7) if cut == QK_CUT else (0,4,7)
            if run == 2 * BANDS - 1: cuts = (0,3,7) if cut == QK_CUT else (0,7)
            return (cuts[cuts.index(c + 1) - 1], c + 1) if c + 1 in cuts else None

        def finish_values(r):
            first, n = units[r]
            acc_v = acc_of[r][2]
            i = 0
            while i < n:
                tiles, c = staged(first + i)
                count = min(n - i, RUN - c)
                nc.vector.tensor_tensor(
                    out=tiles[1][:, :, c : c + count, :].rearrange("p h c d -> p c h d"),
                    in0=acc_v[:, i : i + count, :].rearrange("p c (h d) -> p c h d", h=NH),
                    in1=v_bias[:].rearrange("p (h d) -> p h d", h=NH).unsqueeze(1).to_broadcast(
                        [P, count, NH, DH]
                    ),
                    op=ALU.add,
                )
                i += count
                done = first + i - 1
                part = finished_part(done, V_CUT)
                if part is not None:
                    store(done // RUN, 2, part[0], part[1])

        def turn_back(r, i):
            if i >= units[r][1]:
                return
            tokens = slice(i * P, (i + 1) * P)
            out_ps = psum_r.tile([P, 2, NH, DH], F32, tag="turn")
            for f in range(2):
                for m in range(2):
                    target = out_ps[:, m, :, f * HALF : (f + 1) * HALF]
                    band, c = divmod(units[r][0] + i, WS)
                    if f == 1 and band < BANDS:
                        nc.tensor.matmul(
                            target, lhsT=turned_of[r][f][:, 0, m, tokens],
                            rhs=turns[:, c, :].rearrange("p (h d) -> p h d", h=NH),
                            start=True, stop=True,
                        )
                        continue
                    for k, order in enumerate((ident, swap)):
                        nc.tensor.matmul(
                            target, lhsT=turned_of[r][f][:, k, m, tokens],
                            rhs=order[:].rearrange("p (h d) -> p h d", h=NH),
                            start=k == 0, stop=k == 1, is_transpose=True,
                        )
            turning[r, i] = out_ps

        def leave(r, i):
            if i >= units[r][1]:
                return
            t = units[r][0] + i
            tiles, c = staged(t)
            nc.scalar.copy(out=tiles[0][:, :, :, c, :], in_=turning[r, i][:])
            part = finished_part(t, QK_CUT)
            if part is not None:
                for m in range(2):
                    store(t // RUN, m, part[0], part[1])

        def store(run, n_out, c0, c1):
            qk_stage, v_stage = stage_of[run]
            band, part = divmod(run, 2)
            o = (out_0, out_1, out_2)[n_out]
            if band < BANDS:
                rows = o.rearrange("w h (r c) d -> h w r c d", c=WS)[
                    :, :, band * ROWS : (band + 1) * ROWS, part * RUN + c0 : part * RUN + c1, :
                ]
            else:
                rows = o.rearrange("w h (r c) d -> h w r c d", c=RUN)[
                    :, :, 2 * BANDS * ROWS :, c0:c1, :
                ]
            for h in range(NH):
                src = v_stage[:, h] if n_out == 2 else qk_stage[:, n_out, h]
                nc.sync.dma_start(
                    out=rows[h].rearrange("w r c d -> w r (c d)"),
                    in_=src[:, c0:c1, :].rearrange("p c d -> p (c d)"),
                )

        last = len(units)
        for s in range(last + 4):
            stats, norm, lace, proj, turn = (
                s - lag if 0 <= s - lag < last else None for lag in range(5)
            )
            if proj is not None:
                quantise(proj)
                project(proj)
            if norm is not None:
                normalise(norm)
            if lace is not None:
                interleave(lace)
            if stats is not None:
                statistics(stats, 0)
                statistics(stats, 1)
            if turn is not None and s <= last:
                finish_values(turn)
            if stats is not None:
                finish_statistics(stats)
            if proj is not None:
                rotate_rows(proj, 0)
                rotate_columns(proj)
                rotate_rows(proj, 1)
                if s >= last:
                    finish_values(proj)
            if 2 <= s < 2 + WS // 2:
                make_turns(units[s - 2][0], units[s - 2][0] + 2)
            if turn is not None:
                turn_back(turn, 0)
                leave(turn, 0)
            if stats is not None:
                invert_deviation(stats)
                negate_mean(stats)
            if s == 0:
                q_bias, v_bias = spread_biases(nc, keep, psum_t, ident, bias_rows, vrow, ones)
                group_weights(nc, w_grouped, raw)
            if norm is not None:
                transpose_slots(norm)
            if turn is not None:
                turn_back(turn, 1)
                leave(turn, 1)
            if s == 1:
                nc.vector.tensor_copy(
                    out=perm_last[:].rearrange("p (bi j rl hf) -> p bi j rl hf", bi=8, j=4, rl=2),
                    in_=ident[:].rearrange("p (rl j hf bi) -> p bi j rl hf", rl=2, j=4, hf=2),
                )
                by_row, last_col, pair_col = rotary_tables(nc, keep, setup, by_col, parity, sign)
                w_codes, w_scales = quantise_weights(nc, keep, w_grouped)
